import numpy as np
import ml_dtypes


def mxq(x, axis, fmt="e4m3"):
    dtype, down = {"e4m3": (ml_dtypes.float8_e4m3fn, 7), "e5m2": (ml_dtypes.float8_e5m2, 14)}[fmt]
    v = np.moveaxis(np.asarray(x, np.float32).astype(ml_dtypes.bfloat16).astype(np.float64), axis, -1)
    blocks = v.reshape(v.shape[:-1] + (-1, 32))
    amax = np.abs(blocks).max(-1, keepdims=True)
    byte = np.maximum(np.where(amax > 0, np.frexp(amax)[1] - 1 + 127, 0) - down, 1)
    scale = np.exp2(byte - 127.0)
    codes = (blocks / scale).astype(np.float32).astype(dtype).astype(np.float64)
    return np.moveaxis((codes * scale).reshape(v.shape), -1, axis)


WIDE = False


def mx_kscale(k):
    if not WIDE:
        return np.ones(k)
    levels = np.array([10, -10, 5, -5, 0])
    a = np.random.permutation(np.resize(levels, k // 512 * 4)).reshape(k // 512, 4)
    idx = np.arange(k)
    return np.exp2(a[idx // 512, idx % 128 // 32])


BF16 = ml_dtypes.bfloat16


def bf(x):
    return np.asarray(x, np.float32).astype(BF16)


def f64(x):
    return np.asarray(x).astype(np.float64)


B, C, H, W, P, DIM = 8, 8, 128, 128, 16, 768
SHIFT = P // 2
WD = 5 * C * P * P // 4
N = (H // P) * (W // P)
EPS = 1e-5
XS = 0.015


def patch_shift(x, shift):
    xp = np.pad(x, ((0, 0), (0, 0), (shift, shift), (shift, shift)))
    s2 = 2 * shift
    return np.concatenate([x, xp[:, :, :-s2, :-s2], xp[:, :, :-s2, s2:], xp[:, :, s2:, :-s2], xp[:, :, s2:, s2:]], axis=1)


def haar_detail_mean(x):
    b_, c_, h, w = x.shape
    r = x.reshape(b_, c_, h // 2, 2, w // 2, 2)
    return (3.0 * r[:, :, :, 0, :, 0] - r[:, :, :, 0, :, 1] - r[:, :, :, 1, :, 0] - r[:, :, :, 1, :, 1]) / 6.0


def patchify(x, p):
    b_, c_, hh, ww = x.shape
    h, w = hh // p, ww // p
    return x.reshape(b_, c_, h, p, w, p).transpose(0, 2, 4, 3, 5, 1).reshape(b_, h * w, p * p * c_)


def layernorm(u, g, b):
    m = u.mean(-1, keepdims=True)
    v = np.square(u - m).mean(-1, keepdims=True)
    return (u - m) / np.sqrt(v + EPS) * g + b


def setup_inputs():
    s = mx_kscale(WD)
    return {"x": bf(np.random.standard_normal((B, C, H, W)) * XS),
            "ln2_g": bf((1.0 + 0.1 * np.random.standard_normal(WD)) * s),
            "ln2_b": bf(0.1 * np.random.standard_normal(WD) * s),
            "w2": bf(np.random.standard_normal((WD, DIM)) / np.sqrt(WD) / s[:, None]),
            "b2": bf(0.3 * np.random.standard_normal(DIM)),
            "tok": bf(np.random.standard_normal((B, N, DIM)))}


def reference(x, ln2_g, ln2_b, w2, b2, tok):
    waves = haar_detail_mean(patch_shift(f64(x), SHIFT))
    z = layernorm(patchify(waves, P // 2), f64(ln2_g), f64(ln2_b))
    wtok = (mxq(z, 2, "e4m3") @ mxq(f64(w2), 0, "e4m3")) + f64(b2)
    return f64(tok) + wtok

@@ -1,0 +1,302 @@
+from contextlib import ExitStack
+
+import concourse.mybir as mybir
+from concourse.masks import make_identity
+
+F32 = mybir.dt.float32
+BF16 = mybir.dt.bfloat16
+U32 = mybir.dt.uint32
+U8 = mybir.dt.uint8
+FP8X4 = mybir.dt.float8_e4m3fn_x4
+ALU = mybir.AluOpType
+ACT = mybir.ActivationFunctionType
+AX = mybir.AxisListType
+
+P = 128
+BATCH = 8
+CH = 8
+BANDS = 16
+BAND_ROWS = 4
+DETAIL_W = 64
+PAD = 4
+PADDED_W = DETAIL_W + 2 * PAD
+ROW_LEN = PADDED_W * CH
+BAND_LEN = BAND_ROWS * ROW_LEN
+GRID = 8
+PATCH = 8
+VIEWS = 5
+HALF_K = BAND_ROWS * PATCH * VIEWS * CH
+K = 2 * HALF_K
+DIM = 768
+TOKENS = BATCH * GRID * GRID
+SLOTS = K // P
+PACK = 4
+PASSES = SLOTS // PACK
+HALF_SLOTS = HALF_K // P
+J_GROUP = 4
+J_GROUPS = GRID // J_GROUP
+GROUP_TOKENS = TOKENS // J_GROUPS
+N_WIDE = 512
+HAAR_SCALE = 6.0
+EPS = 1e-5 * HAAR_SCALE * HAAR_SCALE
+
+FLOPS = 2 * TOKENS * K * DIM
+
+
+def tile_shiftedpatchtokenization_pb_kernel(tc, x, ln2_g, ln2_b, w2, b2, tok, out):
+    nc = tc.nc
+    with ExitStack() as ctx:
+        keep = ctx.enter_context(tc.tile_pool(name="keep", bufs=1))
+        w_raw_pool = ctx.enter_context(tc.tile_pool(name="w_raw", bufs=PASSES))
+        w_grp_pool = ctx.enter_context(tc.tile_pool(name="w_grp", bufs=2))
+        z_grp_pool = ctx.enter_context(tc.tile_pool(name="z_grp", bufs=3))
+        small_psum = ctx.enter_context(tc.psum_pool(name="small_psum", bufs=1))
+        turn_psum = ctx.enter_context(tc.psum_pool(name="turn_psum", bufs=4))
+        acc_psum = ctx.enter_context(tc.psum_pool(name="acc_psum", bufs=1))
+
+        image = keep.tile([P, CH, 8 * 128], BF16, tag="image")
+        for c in range(CH):
+            nc.sync.dma_start(
+                out=image[:, c, :],
+                in_=x[:, c, :, :].rearrange("b (a r) w -> a b (r w)", a=BANDS),
+            )
+
+        w_by_pass = w2.rearrange("(g t p) n -> g p t n", t=PACK, p=P)
+        w_raws = []
+        for g in range(PASSES):
+            w_raw = w_raw_pool.tile([P, PACK, DIM], BF16)
+            nc.sync.dma_start(out=w_raw[:], in_=w_by_pass[g])
+            w_raws.append(w_raw)
+
+        gain_rows = keep.tile([P, P], BF16)
+        nc.vector.memset(gain_rows[:], 0.0)
+        nc.scalar.dma_start(out=gain_rows[0:SLOTS, :], in_=ln2_g.rearrange("(s p) -> s p", p=P))
+        nc.scalar.dma_start(out=gain_rows[32 : 32 + SLOTS, :], in_=ln2_b.rearrange("(s p) -> s p", p=P))
+
+        def token_rows(dram, m):
+            jq, bh = divmod(m, 2)
+            rows = dram[4 * bh : 4 * bh + 4, :, :]
+            return rows.rearrange("b (i q j) d -> q (b i) j d", q=J_GROUPS, j=J_GROUP)[jq]
+
+        bias_all = keep.tile([P, DIM], BF16)
+        nc.scalar.dma_start(out=bias_all[:], in_=b2.partition_broadcast(P))
+        tok_in = keep.tile([P, 4, DIM], BF16)
+        for m in range(4):
+            nc.scalar.dma_start(out=tok_in[:, m, :], in_=token_rows(tok, m))
+
+        ident = keep.tile([P, P], F32)
+        make_identity(nc, ident[:])
+        ident_ihb = ident[:].rearrange("p (i h b) -> p i h b", i=GRID, h=2)
+
+        turn_order = keep.tile([P, P], F32)
+        nc.vector.tensor_copy(
+            out=turn_order[:].rearrange("p (h b i) -> p h b i", h=2, b=BATCH),
+            in_=ident[:].rearrange("p (i h b) -> p h b i", i=GRID, h=2),
+        )
+
+        own_bands = keep.tile([P, GRID, BATCH], F32)
+        near_bands = keep.tile([P, GRID, BATCH], F32)
+        nc.vector.tensor_tensor(out=own_bands[:], in0=ident_ihb[:, :, 0, :], in1=ident_ihb[:, :, 1, :], op=ALU.add)
+        nc.vector.tensor_copy(out=near_bands[:, 0:1, :], in_=own_bands[:, 0:1, :])
+        nc.vector.tensor_tensor(
+            out=near_bands[:, 1:GRID, :], in0=own_bands[:, 1:GRID, :], in1=ident_ihb[:, 0 : GRID - 1, 1, :], op=ALU.add
+        )
+        nc.vector.tensor_tensor(
+            out=near_bands[:, 0 : GRID - 1, :], in0=near_bands[:, 0 : GRID - 1, :], in1=ident_ihb[:, 1:GRID, 0, :], op=ALU.add
+        )
+        sum_own = keep.tile([P, P], F32)
+        sum_near = keep.tile([P, P], F32)
+        nc.vector.tensor_copy(
+            out=sum_own[:].rearrange("p (i h b) -> p i h b", i=GRID, h=2),
+            in_=own_bands[:].unsqueeze(2).to_broadcast([P, GRID, 2, BATCH]),
+        )
+        nc.vector.tensor_copy(
+            out=sum_near[:].rearrange("p (i h b) -> p i h b", i=GRID, h=2),
+            in_=near_bands[:].unsqueeze(2).to_broadcast([P, GRID, 2, BATCH]),
+        )
+
+        gain_f32 = keep.tile([P, P], F32)
+        nc.vector.tensor_copy(out=gain_f32[:], in_=gain_rows[:])
+        gain_ps = small_psum.tile([P, P], F32, tag="small")
+        nc.tensor.transpose(out=gain_ps[:], in_=gain_f32[:], identity=ident[:])
+        gain_t = keep.tile([P, P], F32)
+        nc.vector.tensor_copy(out=gain_t[:], in_=gain_ps[:])
+
+        tok_bias = keep.tile([P, 4, DIM], F32)
+        for m in range(4):
+            nc.gpsimd.tensor_tensor(out=tok_bias[:, m, :], in0=tok_in[:, m, :], in1=bias_all[:], op=ALU.add)
+
+        detail = keep.tile([P, BAND_ROWS, PADDED_W, CH], F32)
+        detail_up = keep.tile([P, BAND_ROWS, PADDED_W, CH], F32)
+        detail_dn = keep.tile([P, BAND_ROWS, PADDED_W, CH], F32)
+        nc.gpsimd.memset(detail[:, :, 0:PAD, :], 0.0)
+        nc.gpsimd.memset(detail[:, :, PAD + DETAIL_W : PADDED_W, :], 0.0)
+        zero_rows = keep.tile([BATCH, BAND_LEN], F32)
+        nc.gpsimd.memset(zero_rows[:], 0.0)
+
+        scratch = out.rearrange("b n d -> (b n d)")[0 : (P + 2 * BATCH) * BAND_LEN].rearrange("(q f) -> q f", f=BAND_LEN)
+        nc.sync.dma_start(out=scratch[0:BATCH, :], in_=zero_rows[:])
+        nc.sync.dma_start(out=scratch[P + BATCH : P + 2 * BATCH, :], in_=zero_rows[:])
+
+        pixels = image[:].rearrange("p c (r u j v) -> p c r u j v", r=BAND_ROWS, u=2, j=DETAIL_W, v=2)
+        top = keep.tile([P, CH, BAND_ROWS, DETAIL_W], F32, tag="top")
+        bottom = keep.tile([P, CH, BAND_ROWS, DETAIL_W], F32)
+        for c in range(0, CH, 2):
+            nc.vector.scalar_tensor_tensor(
+                out=top[:, c : c + 2, :, :],
+                in0=pixels[:, c : c + 2, :, 0, :, 0],
+                scalar=3.0,
+                in1=pixels[:, c : c + 2, :, 0, :, 1],
+                op0=ALU.mult,
+                op1=ALU.subtract,
+            )
+            nc.vector.tensor_tensor(
+                out=bottom[:, c : c + 2, :, :],
+                in0=pixels[:, c : c + 2, :, 1, :, 0],
+                in1=pixels[:, c : c + 2, :, 1, :, 1],
+                op=ALU.add,
+            )
+        for r in range(BAND_ROWS):
+            nc.vector.tensor_tensor(
+                out=detail[:, r, PAD : PAD + DETAIL_W, :],
+                in0=top[:, :, r, :].rearrange("p c j -> p j c"),
+                in1=bottom[:, :, r, :].rearrange("p c j -> p j c"),
+                op=ALU.subtract,
+            )
+            cols = slice(r * ROW_LEN, (r + 1) * ROW_LEN)
+            nc.sync.dma_start(out=scratch[BATCH : BATCH + P, cols], in_=detail[:, r, :, :].rearrange("p j c -> p (j c)"))
+        for r in range(BAND_ROWS):
+            cols = slice(r * ROW_LEN, (r + 1) * ROW_LEN)
+            nc.sync.dma_start(out=detail_up[:, r, :, :].rearrange("p j c -> p (j c)"), in_=scratch[0:P, cols])
+            nc.sync.dma_start(out=detail_dn[:, r, :, :].rearrange("p j c -> p (j c)"), in_=scratch[2 * BATCH : 2 * BATCH + P, cols])
+
+        w_codes = keep.tile([P, PASSES, DIM], U32, align_bytes=64)
+        w_scales = keep.tile([P, PASSES, DIM], U8, align_bytes=64)
+        for g in range(PASSES):
+            w_raw = w_raws[g]
+            w_grp = w_grp_pool.tile([P, DIM, PACK], BF16, align_bytes=64)
+            nc.vector.tensor_copy(out=w_grp[:, 0:N_WIDE, :], in_=w_raw[:, :, 0:N_WIDE].rearrange("p t n -> p n t"))
+            nc.scalar.copy(out=w_grp[:, N_WIDE:DIM, :], in_=w_raw[:, :, N_WIDE:DIM].rearrange("p t n -> p n t"))
+            for cols in (slice(0, N_WIDE), slice(N_WIDE, DIM)):
+                nc.vector.quantize_mx(
+                    out=w_codes[:, g, cols].bitcast(FP8X4),
+                    scales=w_scales[:, g, cols],
+                    in_=w_grp[:, cols, :].rearrange("p n t -> p (n t)"),
+                )
+
+        squares = keep.tile([P, BAND_ROWS, DETAIL_W * CH], F32, tag="top")
+        nc.scalar.activation(
+            out=squares[:], in_=detail[:, :, PAD : PAD + DETAIL_W, :].rearrange("p r j c -> p r (j c)"), func=ACT.Square
+        )
+        strip_sums = keep.tile([P, 2, 18], F32)
+        nc.vector.memset(strip_sums[:], 0.0)
+        nc.vector.tensor_reduce(
+            out=strip_sums[:, 0, 1:17],
+            in_=detail[:, :, PAD : PAD + DETAIL_W, :].rearrange("p r (e l) c -> p e r (l c)", l=PAD),
+            axis=AX.XY,
+            op=ALU.add,
+        )
+        nc.vector.tensor_reduce(
+            out=strip_sums[:, 1, 1:17],
+            in_=squares[:].rearrange("p r (e f) -> p e r f", f=PAD * CH),
+            axis=AX.XY,
+            op=ALU.add,
+        )
+        window_sums = keep.tile([P, 2, 2, GRID], F32)
+        inner = strip_sums[:, :, 1:17].rearrange("p q (j v) -> p q j v", v=2)
+        left = strip_sums[:, :, 0:16].rearrange("p q (j v) -> p q j v", v=2)
+        right = strip_sums[:, :, 2:18].rearrange("p q (j v) -> p q j v", v=2)
+        nc.vector.tensor_tensor(out=window_sums[:, 0, :, :], in0=inner[:, :, :, 0], in1=inner[:, :, :, 1], op=ALU.add)
+        nc.vector.tensor_tensor(out=window_sums[:, 1, :, :], in0=left[:, :, :, 0], in1=right[:, :, :, 1], op=ALU.add)
+        nc.vector.tensor_tensor(out=window_sums[:, 1, :, :], in0=window_sums[:, 1, :, :], in1=window_sums[:, 0, :, :], op=ALU.add)
+        token_sums = small_psum.tile([P, 2 * GRID], F32, tag="small")
+        nc.tensor.matmul(
+            out=token_sums[:], lhsT=sum_own[:], rhs=window_sums[:, 0, :, :].rearrange("p q j -> p (q j)"), start=True, stop=False
+        )
+        nc.tensor.matmul(
+            out=token_sums[:], lhsT=sum_near[:], rhs=window_sums[:, 1, :, :].rearrange("p q j -> p (q j)"), start=False, stop=True
+        )
+        mean = keep.tile([P, GRID], F32)
+        mean_sq = keep.tile([P, GRID], F32)
+        var = keep.tile([P, GRID], F32)
+        std = keep.tile([P, GRID], F32)
+        rstd0 = keep.tile([P, GRID], F32)
+        newton = keep.tile([P, GRID], F32)
+        rstd = keep.tile([P, GRID], F32)
+        shift = keep.tile([P, GRID], F32)
+        nc.vector.tensor_scalar(out=mean[:], in0=token_sums[:, 0:GRID], scalar1=1.0 / K, scalar2=None, op0=ALU.mult)
+        nc.vector.tensor_tensor(out=mean_sq[:], in0=mean[:], in1=mean[:], op=ALU.mult)
+        nc.vector.scalar_tensor_tensor(
+            out=var[:], in0=token_sums[:, GRID : 2 * GRID], scalar=1.0 / K, in1=mean_sq[:], op0=ALU.mult, op1=ALU.subtract
+        )
+        nc.vector.tensor_scalar(out=var[:], in0=var[:], scalar1=EPS, scalar2=None, op0=ALU.add)
+        nc.scalar.activation(out=std[:], in_=var[:], func=ACT.Sqrt)
+        nc.vector.reciprocal(out=rstd0[:], in_=std[:])
+        nc.vector.tensor_tensor(out=newton[:], in0=var[:], in1=rstd0[:], op=ALU.mult)
+        nc.vector.tensor_tensor(out=newton[:], in0=newton[:], in1=rstd0[:], op=ALU.mult)
+        nc.vector.tensor_scalar(out=newton[:], in0=newton[:], scalar1=-0.5, scalar2=1.5, op0=ALU.mult, op1=ALU.add)
+        nc.vector.tensor_tensor(out=rstd[:], in0=rstd0[:], in1=newton[:], op=ALU.mult)
+        nc.vector.scalar_tensor_tensor(out=shift[:], in0=mean[:], scalar=-1.0, in1=rstd[:], op0=ALU.mult, op1=ALU.mult)
+
+        normed = keep.tile([P, GRID, HALF_K], F32)
+        normed_v = normed[:].rearrange("p j (r q s c) -> p j r q s c", r=BAND_ROWS, q=PATCH, s=VIEWS, c=CH)
+        views = ((detail, 0), (detail_up, -PAD), (detail_up, PAD), (detail_dn, -PAD), (detail_dn, PAD))
+        planes = keep.tile([P, SLOTS, J_GROUPS, GROUP_TOKENS], BF16, tag="image")
+        z_codes = keep.tile([P, PASSES, TOKENS], U32, align_bytes=64)
+        z_scales = keep.tile([P, PASSES, TOKENS], U8, align_bytes=64)
+
+        for jq in range(J_GROUPS):
+            for j in range(jq * J_GROUP, (jq + 1) * J_GROUP):
+                for s in range(VIEWS):
+                    source, dx = views[s]
+                    first = PAD + PATCH * j + dx
+                    nc.scalar.activation(
+                        out=normed_v[:, j, :, :, s, :],
+                        in_=source[:, :, first : first + PATCH, :],
+                        func=ACT.Identity,
+                        scale=rstd[:, j : j + 1],
+                        bias=shift[:, j : j + 1],
+                    )
+            for sg in range(HALF_SLOTS):
+                turned = turn_psum.tile([P, J_GROUP, P], F32)
+                for j4 in range(J_GROUP):
+                    nc.tensor.transpose(
+                        out=turned[:, j4, :],
+                        in_=normed[:, jq * J_GROUP + j4, sg * P : (sg + 1) * P],
+                        identity=turn_order[:],
+                    )
+                for h in range(2):
+                    slot = sg + HALF_SLOTS * h
+                    nc.scalar.activation(
+                        out=planes[:, slot, jq, :].rearrange("p (g j) -> p g j", j=J_GROUP),
+                        in_=turned[:, :, 64 * h : 64 * h + 64].rearrange("p j g -> p g j"),
+                        func=ACT.Identity,
+                        scale=gain_t[:, slot : slot + 1],
+                        bias=gain_t[:, 32 + slot : 33 + slot],
+                    )
+            toks = slice(jq * GROUP_TOKENS, (jq + 1) * GROUP_TOKENS)
+            for g in range(PASSES):
+                z_grp = z_grp_pool.tile([P, GROUP_TOKENS, PACK], BF16, align_bytes=64)
+                nc.vector.tensor_copy(out=z_grp[:], in_=planes[:, PACK * g : PACK * (g + 1), jq, :].rearrange("p t w -> p w t"))
+                nc.vector.quantize_mx(
+                    out=z_codes[:, g, toks].bitcast(FP8X4),
+                    scales=z_scales[:, g, toks],
+                    in_=z_grp[:].rearrange("p w t -> p (w t)"),
+                )
+            for m in (2 * jq, 2 * jq + 1):
+                rows = slice(m * P, (m + 1) * P)
+                acc_wide = acc_psum.tile([P, N_WIDE], F32)
+                acc_rest = acc_psum.tile([P, DIM - N_WIDE], F32)
+                for acc, cols in ((acc_wide, slice(0, N_WIDE)), (acc_rest, slice(N_WIDE, DIM))):
+                    for g in range(PASSES):
+                        nc.tensor.matmul_mx(
+                            out=acc[:],
+                            lhsT=z_codes[:, g, rows].bitcast(FP8X4),
+                            lhsT_scale=z_scales[:, g, rows],
+                            rhs=w_codes[:, g, cols].bitcast(FP8X4),
+                            rhs_scale=w_scales[:, g, cols],
+                            start=(g == 0),
+                            stop=(g == PASSES - 1),
+                        )
+                    nc.vector.tensor_tensor(out=tok_bias[:, m, cols], in0=acc[:], in1=tok_bias[:, m, cols], op=ALU.add)
+                nc.sync.dma_start(out=token_rows(out, m), in_=tok_bias[:, m, :])

@@ -37,6 +37,7 @@ J_GROUP = 4
 J_GROUPS = GRID // J_GROUP
 GROUP_TOKENS = TOKENS // J_GROUPS
 N_WIDE = 512
+EARLY_W = 3
 HAAR_SCALE = 6.0
 EPS = 1e-5 * HAAR_SCALE * HAAR_SCALE
 
@@ -52,7 +53,8 @@ def tile_shiftedpatchtokenization_pb_kernel(tc, x, ln2_g, ln2_b, w2, b2, tok, ou
         z_grp_pool = ctx.enter_context(tc.tile_pool(name="z_grp", bufs=3))
         small_psum = ctx.enter_context(tc.psum_pool(name="small_psum", bufs=1))
         turn_psum = ctx.enter_context(tc.psum_pool(name="turn_psum", bufs=4))
-        acc_psum = ctx.enter_context(tc.psum_pool(name="acc_psum", bufs=1))
+        wide_psum = ctx.enter_context(tc.psum_pool(name="wide_psum", bufs=2))
+        rest_psum = ctx.enter_context(tc.psum_pool(name="rest_psum", bufs=1))
 
         image = keep.tile([P, CH, 8 * 128], BF16, tag="image")
         for c in range(CH):
@@ -65,8 +67,9 @@ def tile_shiftedpatchtokenization_pb_kernel(tc, x, ln2_g, ln2_b, w2, b2, tok, ou
         w_raws = []
         for g in range(PASSES):
             w_raw = w_raw_pool.tile([P, PACK, DIM], BF16)
-            nc.sync.dma_start(out=w_raw[:], in_=w_by_pass[g])
             w_raws.append(w_raw)
+        for g in range(EARLY_W):
+            nc.sync.dma_start(out=w_raws[g][:], in_=w_by_pass[g])
 
         gain_rows = keep.tile([P, P], BF16)
         nc.vector.memset(gain_rows[:], 0.0)
@@ -79,10 +82,15 @@ def tile_shiftedpatchtokenization_pb_kernel(tc, x, ln2_g, ln2_b, w2, b2, tok, ou
             return rows.rearrange("b (i q j) d -> q (b i) j d", q=J_GROUPS, j=J_GROUP)[jq]
 
         bias_all = keep.tile([P, DIM], BF16)
-        nc.scalar.dma_start(out=bias_all[:], in_=b2.partition_broadcast(P))
+        nc.sync.dma_start(out=bias_all[:], in_=b2.partition_broadcast(P))
         tok_in = keep.tile([P, 4, DIM], BF16)
         for m in range(4):
-            nc.scalar.dma_start(out=tok_in[:, m, :], in_=token_rows(tok, m))
+            nc.sync.dma_start(out=tok_in[:, m, :], in_=token_rows(tok, m))
+
+        one = keep.tile([P, 1], F32)
+        one_root = keep.tile([P, 1], F32)
+        nc.vector.memset(one[:], 1.0)
+        nc.scalar.activation(out=one_root[:], in_=one[:], func=ACT.Sqrt)
 
         ident = keep.tile([P, P], F32)
         make_identity(nc, ident[:])
@@ -123,8 +131,6 @@ def tile_shiftedpatchtokenization_pb_kernel(tc, x, ln2_g, ln2_b, w2, b2, tok, ou
         nc.vector.tensor_copy(out=gain_t[:], in_=gain_ps[:])
 
         tok_bias = keep.tile([P, 4, DIM], F32)
-        for m in range(4):
-            nc.gpsimd.tensor_tensor(out=tok_bias[:, m, :], in0=tok_in[:, m, :], in1=bias_all[:], op=ALU.add)
 
         detail = keep.tile([P, BAND_ROWS, PADDED_W, CH], F32)
         detail_up = keep.tile([P, BAND_ROWS, PADDED_W, CH], F32)
@@ -139,66 +145,51 @@ def tile_shiftedpatchtokenization_pb_kernel(tc, x, ln2_g, ln2_b, w2, b2, tok, ou
         nc.sync.dma_start(out=scratch[P + BATCH : P + 2 * BATCH, :], in_=zero_rows[:])
 
         pixels = image[:].rearrange("p c (r u j v) -> p c r u j v", r=BAND_ROWS, u=2, j=DETAIL_W, v=2)
-        top = keep.tile([P, CH, BAND_ROWS, DETAIL_W], F32, tag="top")
+        by_channel = keep.tile([P, CH, BAND_ROWS, DETAIL_W], F32)
         bottom = keep.tile([P, CH, BAND_ROWS, DETAIL_W], F32)
+        squares = keep.tile([P, CH, BAND_ROWS, DETAIL_W], F32)
         for c in range(0, CH, 2):
+            pair = slice(c, c + 2)
             nc.vector.scalar_tensor_tensor(
-                out=top[:, c : c + 2, :, :],
-                in0=pixels[:, c : c + 2, :, 0, :, 0],
+                out=by_channel[:, pair, :, :],
+                in0=pixels[:, pair, :, 0, :, 0],
                 scalar=3.0,
-                in1=pixels[:, c : c + 2, :, 0, :, 1],
+                in1=pixels[:, pair, :, 0, :, 1],
                 op0=ALU.mult,
                 op1=ALU.subtract,
             )
             nc.vector.tensor_tensor(
-                out=bottom[:, c : c + 2, :, :],
-                in0=pixels[:, c : c + 2, :, 1, :, 0],
-                in1=pixels[:, c : c + 2, :, 1, :, 1],
-                op=ALU.add,
+                out=bottom[:, pair, :, :], in0=pixels[:, pair, :, 1, :, 0], in1=pixels[:, pair, :, 1, :, 1], op=ALU.add
             )
-        for r in range(BAND_ROWS):
             nc.vector.tensor_tensor(
-                out=detail[:, r, PAD : PAD + DETAIL_W, :],
-                in0=top[:, :, r, :].rearrange("p c j -> p j c"),
-                in1=bottom[:, :, r, :].rearrange("p c j -> p j c"),
-                op=ALU.subtract,
+                out=by_channel[:, pair, :, :], in0=by_channel[:, pair, :, :], in1=bottom[:, pair, :, :], op=ALU.subtract
+            )
+            nc.scalar.activation(out=squares[:, pair, :, :], in_=by_channel[:, pair, :, :], func=ACT.Square)
+        for r in range(BAND_ROWS):
+            nc.scalar.copy(
+                out=detail[:, r, PAD : PAD + DETAIL_W, :].rearrange("p j (h c) -> p h j c", h=2),
+                in_=by_channel[:, :, r, :].rearrange("p (h c) j -> p h j c", h=2),
             )
             cols = slice(r * ROW_LEN, (r + 1) * ROW_LEN)
-            nc.sync.dma_start(out=scratch[BATCH : BATCH + P, cols], in_=detail[:, r, :, :].rearrange("p j c -> p (j c)"))
+            nc.scalar.dma_start(out=scratch[BATCH : BATCH + P, cols], in_=detail[:, r, :, :].rearrange("p j c -> p (j c)"))
         for r in range(BAND_ROWS):
             cols = slice(r * ROW_LEN, (r + 1) * ROW_LEN)
             nc.sync.dma_start(out=detail_up[:, r, :, :].rearrange("p j c -> p (j c)"), in_=scratch[0:P, cols])
             nc.sync.dma_start(out=detail_dn[:, r, :, :].rearrange("p j c -> p (j c)"), in_=scratch[2 * BATCH : 2 * BATCH + P, cols])
+        for g in range(EARLY_W, PASSES):
+            nc.sync.dma_start(out=w_raws[g][:], in_=w_by_pass[g])
 
-        w_codes = keep.tile([P, PASSES, DIM], U32, align_bytes=64)
-        w_scales = keep.tile([P, PASSES, DIM], U8, align_bytes=64)
-        for g in range(PASSES):
-            w_raw = w_raws[g]
-            w_grp = w_grp_pool.tile([P, DIM, PACK], BF16, align_bytes=64)
-            nc.vector.tensor_copy(out=w_grp[:, 0:N_WIDE, :], in_=w_raw[:, :, 0:N_WIDE].rearrange("p t n -> p n t"))
-            nc.scalar.copy(out=w_grp[:, N_WIDE:DIM, :], in_=w_raw[:, :, N_WIDE:DIM].rearrange("p t n -> p n t"))
-            for cols in (slice(0, N_WIDE), slice(N_WIDE, DIM)):
-                nc.vector.quantize_mx(
-                    out=w_codes[:, g, cols].bitcast(FP8X4),
-                    scales=w_scales[:, g, cols],
-                    in_=w_grp[:, cols, :].rearrange("p n t -> p (n t)"),
-                )
-
-        squares = keep.tile([P, BAND_ROWS, DETAIL_W * CH], F32, tag="top")
-        nc.scalar.activation(
-            out=squares[:], in_=detail[:, :, PAD : PAD + DETAIL_W, :].rearrange("p r j c -> p r (j c)"), func=ACT.Square
-        )
         strip_sums = keep.tile([P, 2, 18], F32)
         nc.vector.memset(strip_sums[:], 0.0)
         nc.vector.tensor_reduce(
             out=strip_sums[:, 0, 1:17],
-            in_=detail[:, :, PAD : PAD + DETAIL_W, :].rearrange("p r (e l) c -> p e r (l c)", l=PAD),
+            in_=by_channel[:].rearrange("p c r (e l) -> p e (c r) l", l=PAD),
             axis=AX.XY,
             op=ALU.add,
         )
         nc.vector.tensor_reduce(
             out=strip_sums[:, 1, 1:17],
-            in_=squares[:].rearrange("p r (e f) -> p e r f", f=PAD * CH),
+            in_=squares[:].rearrange("p c r (e l) -> p e (c r) l", l=PAD),
             axis=AX.XY,
             op=ALU.add,
         )
@@ -216,6 +207,10 @@ def tile_shiftedpatchtokenization_pb_kernel(tc, x, ln2_g, ln2_b, w2, b2, tok, ou
         nc.tensor.matmul(
             out=token_sums[:], lhsT=sum_near[:], rhs=window_sums[:, 1, :, :].rearrange("p q j -> p (q j)"), start=False, stop=True
         )
+        def add_bias(m):
+            nc.vector.tensor_tensor(out=tok_bias[:, m, :], in0=tok_in[:, m, :], in1=bias_all[:], op=ALU.add)
+
+        add_bias(0)
         mean = keep.tile([P, GRID], F32)
         mean_sq = keep.tile([P, GRID], F32)
         var = keep.tile([P, GRID], F32)
@@ -231,12 +226,30 @@ def tile_shiftedpatchtokenization_pb_kernel(tc, x, ln2_g, ln2_b, w2, b2, tok, ou
         )
         nc.vector.tensor_scalar(out=var[:], in0=var[:], scalar1=EPS, scalar2=None, op0=ALU.add)
         nc.scalar.activation(out=std[:], in_=var[:], func=ACT.Sqrt)
+        add_bias(1)
         nc.vector.reciprocal(out=rstd0[:], in_=std[:])
         nc.vector.tensor_tensor(out=newton[:], in0=var[:], in1=rstd0[:], op=ALU.mult)
         nc.vector.tensor_tensor(out=newton[:], in0=newton[:], in1=rstd0[:], op=ALU.mult)
         nc.vector.tensor_scalar(out=newton[:], in0=newton[:], scalar1=-0.5, scalar2=1.5, op0=ALU.mult, op1=ALU.add)
         nc.vector.tensor_tensor(out=rstd[:], in0=rstd0[:], in1=newton[:], op=ALU.mult)
         nc.vector.scalar_tensor_tensor(out=shift[:], in0=mean[:], scalar=-1.0, in1=rstd[:], op0=ALU.mult, op1=ALU.mult)
+        add_bias(2)
+        add_bias(3)
+
+        w_codes = keep.tile([P, PASSES, DIM], U32, align_bytes=64)
+        w_scales = keep.tile([P, PASSES, DIM], U8, align_bytes=64)
+        for g in range(PASSES):
+            w_grp = w_grp_pool.tile([P, DIM, PACK], BF16, align_bytes=64)
+            for cols in (slice(0, N_WIDE), slice(N_WIDE, DIM)):
+                nc.scalar.copy(
+                    out=w_grp[:, cols, :].rearrange("p (n i) t -> p n t i", i=4),
+                    in_=w_raws[g][:, :, cols].rearrange("p t (n i) -> p n t i", i=4),
+                )
+                nc.vector.quantize_mx(
+                    out=w_codes[:, g, cols].bitcast(FP8X4),
+                    scales=w_scales[:, g, cols],
+                    in_=w_grp[:, cols, :].rearrange("p n t -> p (n t)"),
+                )
 
         normed = keep.tile([P, GRID, HALF_K], F32)
         normed_v = normed[:].rearrange("p j (r q s c) -> p j r q s c", r=BAND_ROWS, q=PATCH, s=VIEWS, c=CH)
@@ -246,16 +259,18 @@ def tile_shiftedpatchtokenization_pb_kernel(tc, x, ln2_g, ln2_b, w2, b2, tok, ou
         z_scales = keep.tile([P, PASSES, TOKENS], U8, align_bytes=64)
 
         for jq in range(J_GROUPS):
+            toks = slice(jq * GROUP_TOKENS, (jq + 1) * GROUP_TOKENS)
             for j in range(jq * J_GROUP, (jq + 1) * J_GROUP):
                 for s in range(VIEWS):
                     source, dx = views[s]
                     first = PAD + PATCH * j + dx
-                    nc.scalar.activation(
+                    nc.vector.tensor_scalar(
                         out=normed_v[:, j, :, :, s, :],
-                        in_=source[:, :, first : first + PATCH, :],
-                        func=ACT.Identity,
-                        scale=rstd[:, j : j + 1],
-                        bias=shift[:, j : j + 1],
+                        in0=source[:, :, first : first + PATCH, :],
+                        scalar1=rstd[:, j : j + 1],
+                        scalar2=shift[:, j : j + 1],
+                        op0=ALU.mult,
+                        op1=ALU.add,
                     )
             for sg in range(HALF_SLOTS):
                 turned = turn_psum.tile([P, J_GROUP, P], F32)
@@ -274,19 +289,22 @@ def tile_shiftedpatchtokenization_pb_kernel(tc, x, ln2_g, ln2_b, w2, b2, tok, ou
                         scale=gain_t[:, slot : slot + 1],
                         bias=gain_t[:, 32 + slot : 33 + slot],
                     )
-            toks = slice(jq * GROUP_TOKENS, (jq + 1) * GROUP_TOKENS)
-            for g in range(PASSES):
-                z_grp = z_grp_pool.tile([P, GROUP_TOKENS, PACK], BF16, align_bytes=64)
-                nc.vector.tensor_copy(out=z_grp[:], in_=planes[:, PACK * g : PACK * (g + 1), jq, :].rearrange("p t w -> p w t"))
-                nc.vector.quantize_mx(
-                    out=z_codes[:, g, toks].bitcast(FP8X4),
-                    scales=z_scales[:, g, toks],
-                    in_=z_grp[:].rearrange("p w t -> p (w t)"),
-                )
+                for g in range(PASSES):
+                    if max([(PACK * g + t) % HALF_SLOTS for t in range(PACK)]) == sg:
+                        z_grp = z_grp_pool.tile([P, GROUP_TOKENS, PACK], BF16, align_bytes=64)
+                        nc.vector.tensor_copy(
+                            out=z_grp[:].rearrange("p (w i) t -> p w t i", i=4),
+                            in_=planes[:, PACK * g : PACK * (g + 1), jq, :].rearrange("p t (w i) -> p w t i", i=4),
+                        )
+                        nc.vector.quantize_mx(
+                            out=z_codes[:, g, toks].bitcast(FP8X4),
+                            scales=z_scales[:, g, toks],
+                            in_=z_grp[:].rearrange("p w t -> p (w t)"),
+                        )
             for m in (2 * jq, 2 * jq + 1):
                 rows = slice(m * P, (m + 1) * P)
-                acc_wide = acc_psum.tile([P, N_WIDE], F32)
-                acc_rest = acc_psum.tile([P, DIM - N_WIDE], F32)
+                acc_wide = wide_psum.tile([P, N_WIDE], F32)
+                acc_rest = rest_psum.tile([P, DIM - N_WIDE], F32)
                 for acc, cols in ((acc_wide, slice(0, N_WIDE)), (acc_rest, slice(N_WIDE, DIM))):
                     for g in range(PASSES):
                         nc.tensor.matmul_mx(

@@ -37,7 +37,16 @@ J_GROUP = 4
 J_GROUPS = GRID // J_GROUP
 GROUP_TOKENS = TOKENS // J_GROUPS
 N_WIDE = 512
-EARLY_W = 3
+WIDE = slice(0, N_WIDE)
+REST = slice(N_WIDE, DIM)
+LAST_PLANE = [max([(PACK * g + t) % HALF_SLOTS for t in range(PACK)]) for g in range(PASSES)]
+PASS_ORDER = sorted(range(PASSES), key=lambda g: LAST_PLANE[g])
+STEPS = J_GROUPS * HALF_SLOTS
+TURN_BANKS = 4
+AHEAD = TURN_BANKS - 1
+LAG = 6
+LAST_W_STEP = 6
+EARLY_W = 4
 HAAR_SCALE = 6.0
 EPS = 1e-5 * HAAR_SCALE * HAAR_SCALE
 
@@ -49,59 +58,79 @@ def tile_shiftedpatchtokenization_pb_kernel(tc, x, ln2_g, ln2_b, w2, b2, tok, ou
     with ExitStack() as ctx:
         keep = ctx.enter_context(tc.tile_pool(name="keep", bufs=1))
         w_raw_pool = ctx.enter_context(tc.tile_pool(name="w_raw", bufs=PASSES))
-        w_grp_pool = ctx.enter_context(tc.tile_pool(name="w_grp", bufs=2))
+        w_grp_pool = ctx.enter_context(tc.tile_pool(name="w_grp", bufs=3))
         z_grp_pool = ctx.enter_context(tc.tile_pool(name="z_grp", bufs=3))
-        small_psum = ctx.enter_context(tc.psum_pool(name="small_psum", bufs=1))
-        turn_psum = ctx.enter_context(tc.psum_pool(name="turn_psum", bufs=4))
-        wide_psum = ctx.enter_context(tc.psum_pool(name="wide_psum", bufs=2))
-        rest_psum = ctx.enter_context(tc.psum_pool(name="rest_psum", bufs=1))
+        turn_psum = ctx.enter_context(tc.psum_pool(name="turn_psum", bufs=TURN_BANKS))
+        acc_psum = ctx.enter_context(tc.psum_pool(name="acc_psum", bufs=1))
+        ctx.enter_context(tc.manual_schedule())
 
         image = keep.tile([P, CH, 8 * 128], BF16, tag="image")
-        for c in range(CH):
-            nc.sync.dma_start(
-                out=image[:, c, :],
-                in_=x[:, c, :, :].rearrange("b (a r) w -> a b (r w)", a=BANDS),
-            )
-
-        w_by_pass = w2.rearrange("(g t p) n -> g p t n", t=PACK, p=P)
         w_raws = []
         for g in range(PASSES):
             w_raw = w_raw_pool.tile([P, PACK, DIM], BF16)
             w_raws.append(w_raw)
-        for g in range(EARLY_W):
-            nc.sync.dma_start(out=w_raws[g][:], in_=w_by_pass[g])
-
-        gain_rows = keep.tile([P, P], BF16)
-        nc.vector.memset(gain_rows[:], 0.0)
-        nc.scalar.dma_start(out=gain_rows[0:SLOTS, :], in_=ln2_g.rearrange("(s p) -> s p", p=P))
-        nc.scalar.dma_start(out=gain_rows[32 : 32 + SLOTS, :], in_=ln2_b.rearrange("(s p) -> s p", p=P))
+        w_by_pass = w2.rearrange("(g t p) n -> g p t n", t=PACK, p=P)
+        w_codes = keep.tile([P, PASSES, DIM], U32, align_bytes=64)
+        w_scales = keep.tile([P, PASSES, DIM], U8, align_bytes=64)
+        z_codes = keep.tile([P, PASSES, TOKENS], U32, align_bytes=64)
+        z_scales = keep.tile([P, PASSES, TOKENS], U8, align_bytes=64)
+        tok_in = keep.tile([P, 4, DIM], BF16)
+        tok_bias = keep.tile([P, 4, DIM], F32)
+        detail = keep.tile([P, BAND_ROWS, PADDED_W, CH], F32)
+        detail_up = keep.tile([P, BAND_ROWS, PADDED_W, CH], F32)
+        detail_dn = keep.tile([P, BAND_ROWS, PADDED_W, CH], F32)
+        scratch = out.rearrange("b n d -> (b n d)")[0 : (P + 2 * BATCH) * BAND_LEN].rearrange("(q f) -> q f", f=BAND_LEN)
 
         def token_rows(dram, m):
             jq, bh = divmod(m, 2)
             rows = dram[4 * bh : 4 * bh + 4, :, :]
             return rows.rearrange("b (i q j) d -> q (b i) j d", q=J_GROUPS, j=J_GROUP)[jq]
 
-        bias_all = keep.tile([P, DIM], BF16)
-        nc.sync.dma_start(out=bias_all[:], in_=b2.partition_broadcast(P))
-        tok_in = keep.tile([P, 4, DIM], BF16)
-        for m in range(4):
-            nc.sync.dma_start(out=tok_in[:, m, :], in_=token_rows(tok, m))
+        def load_image(c):
+            nc.sync.dma_start(out=image[:, c, :], in_=x[:, c, :, :].rearrange("b (a r) w -> a b (r w)", a=BANDS))
 
+        def load_w(g):
+            nc.sync.dma_start(out=w_raws[g][:], in_=w_by_pass[g])
+
+        gain_rows = keep.tile([P, P], BF16)
+        bias_row = keep.tile([P, DIM], BF16)
+        ones = keep.tile([P, P], BF16)
         one = keep.tile([P, 1], F32)
         one_root = keep.tile([P, 1], F32)
+        zero_rows = keep.tile([BATCH, BAND_LEN], F32, tag="normed")
+        nc.vector.memset(gain_rows[:], 0.0)
+        nc.vector.memset(zero_rows[:], 0.0)
+        nc.vector.memset(bias_row[:], 0.0)
+        nc.vector.memset(ones[:], 1.0)
         nc.vector.memset(one[:], 1.0)
+        nc.scalar.dma_start(out=gain_rows[0:SLOTS, :], in_=ln2_g.rearrange("(s p) -> s p", p=P))
+        nc.scalar.dma_start(out=gain_rows[32 : 32 + SLOTS, :], in_=ln2_b.rearrange("(s p) -> s p", p=P))
+        nc.scalar.dma_start(out=bias_row[0:1, :], in_=b2.unsqueeze(0))
+        nc.scalar.dma_start(out=scratch[0:BATCH, :], in_=zero_rows[:])
+        nc.scalar.dma_start(out=scratch[P + BATCH : P + 2 * BATCH, :], in_=zero_rows[:])
+        for c in range(4):
+            load_image(c)
+        load_w(PASS_ORDER[0])
+        for c in range(4, CH):
+            load_image(c)
+        for m in range(4):
+            nc.sync.dma_start(out=tok_in[:, m, :], in_=token_rows(tok, m))
+        for g in PASS_ORDER[1:EARLY_W]:
+            load_w(g)
+
         nc.scalar.activation(out=one_root[:], in_=one[:], func=ACT.Sqrt)
 
         ident = keep.tile([P, P], F32)
         make_identity(nc, ident[:])
-        ident_ihb = ident[:].rearrange("p (i h b) -> p i h b", i=GRID, h=2)
+        nc.gpsimd.memset(detail[:, :, 0:PAD, :], 0.0)
+        nc.gpsimd.memset(detail[:, :, PAD + DETAIL_W : PADDED_W, :], 0.0)
 
+        ident_ihb = ident[:].rearrange("p (i h b) -> p i h b", i=GRID, h=2)
         turn_order = keep.tile([P, P], F32)
         nc.vector.tensor_copy(
             out=turn_order[:].rearrange("p (h b i) -> p h b i", h=2, b=BATCH),
             in_=ident[:].rearrange("p (i h b) -> p h b i", i=GRID, h=2),
         )
-
         own_bands = keep.tile([P, GRID, BATCH], F32)
         near_bands = keep.tile([P, GRID, BATCH], F32)
         nc.vector.tensor_tensor(out=own_bands[:], in0=ident_ihb[:, :, 0, :], in1=ident_ihb[:, :, 1, :], op=ALU.add)
@@ -122,33 +151,51 @@ def tile_shiftedpatchtokenization_pb_kernel(tc, x, ln2_g, ln2_b, w2, b2, tok, ou
             out=sum_near[:].rearrange("p (i h b) -> p i h b", i=GRID, h=2),
             in_=near_bands[:].unsqueeze(2).to_broadcast([P, GRID, 2, BATCH]),
         )
+        strip_sums = keep.tile([P, 2, 18], F32)
+        nc.vector.memset(strip_sums[:], 0.0)
 
         gain_f32 = keep.tile([P, P], F32)
         nc.vector.tensor_copy(out=gain_f32[:], in_=gain_rows[:])
-        gain_ps = small_psum.tile([P, P], F32, tag="small")
+        gain_ps = turn_psum.tile([P, P], F32, tag="turned")
         nc.tensor.transpose(out=gain_ps[:], in_=gain_f32[:], identity=ident[:])
         gain_t = keep.tile([P, P], F32)
         nc.vector.tensor_copy(out=gain_t[:], in_=gain_ps[:])
 
-        tok_bias = keep.tile([P, 4, DIM], F32)
+        bias_wide = acc_psum.tile([P, N_WIDE], F32, tag="wide0")
+        bias_rest = acc_psum.tile([P, DIM - N_WIDE], F32, tag="rest0")
+        nc.tensor.matmul(out=bias_wide[:], lhsT=ones[:], rhs=bias_row[:, 0:N_WIDE], start=True, stop=True)
+        nc.tensor.matmul(out=bias_rest[:], lhsT=ones[:], rhs=bias_row[:, N_WIDE:DIM], start=True, stop=True)
 
-        detail = keep.tile([P, BAND_ROWS, PADDED_W, CH], F32)
-        detail_up = keep.tile([P, BAND_ROWS, PADDED_W, CH], F32)
-        detail_dn = keep.tile([P, BAND_ROWS, PADDED_W, CH], F32)
-        nc.gpsimd.memset(detail[:, :, 0:PAD, :], 0.0)
-        nc.gpsimd.memset(detail[:, :, PAD + DETAIL_W : PADDED_W, :], 0.0)
-        zero_rows = keep.tile([BATCH, BAND_LEN], F32)
-        nc.gpsimd.memset(zero_rows[:], 0.0)
+        def add_bias(m):
+            nc.vector.tensor_tensor(out=tok_bias[:, m, 0:N_WIDE], in0=bias_wide[:], in1=tok_in[:, m, 0:N_WIDE], op=ALU.add)
+            nc.vector.tensor_tensor(out=tok_bias[:, m, N_WIDE:DIM], in0=bias_rest[:], in1=tok_in[:, m, N_WIDE:DIM], op=ALU.add)
 
-        scratch = out.rearrange("b n d -> (b n d)")[0 : (P + 2 * BATCH) * BAND_LEN].rearrange("(q f) -> q f", f=BAND_LEN)
-        nc.sync.dma_start(out=scratch[0:BATCH, :], in_=zero_rows[:])
-        nc.sync.dma_start(out=scratch[P + BATCH : P + 2 * BATCH, :], in_=zero_rows[:])
+        w_grps = {}
+
+        def regroup_w(g, cols):
+            if g not in w_grps:
+                w_grp = w_grp_pool.tile([P, DIM, PACK], BF16, align_bytes=64)
+                w_grps[g] = w_grp
+            grouped = w_grps[g][:, cols, :].rearrange("p (n i) t -> p n t i", i=4)
+            rows = w_raws[g][:, :, cols].rearrange("p t (n i) -> p n t i", i=4)
+            if g == PASS_ORDER[-1]:
+                nc.vector.tensor_copy(out=grouped, in_=rows)
+            else:
+                nc.scalar.copy(out=grouped, in_=rows)
+
+        def quantise_w(g):
+            for cols in (WIDE, REST):
+                nc.vector.quantize_mx(
+                    out=w_codes[:, g, cols].bitcast(FP8X4),
+                    scales=w_scales[:, g, cols],
+                    in_=w_grps[g][:, cols, :].rearrange("p n t -> p (n t)"),
+                )
 
         pixels = image[:].rearrange("p c (r u j v) -> p c r u j v", r=BAND_ROWS, u=2, j=DETAIL_W, v=2)
         by_channel = keep.tile([P, CH, BAND_ROWS, DETAIL_W], F32)
         bottom = keep.tile([P, CH, BAND_ROWS, DETAIL_W], F32)
         squares = keep.tile([P, CH, BAND_ROWS, DETAIL_W], F32)
-        for c in range(0, CH, 2):
+        def rows_of_blocks(c):
             pair = slice(c, c + 2)
             nc.vector.scalar_tensor_tensor(
                 out=by_channel[:, pair, :, :],
@@ -161,37 +208,44 @@ def tile_shiftedpatchtokenization_pb_kernel(tc, x, ln2_g, ln2_b, w2, b2, tok, ou
             nc.vector.tensor_tensor(
                 out=bottom[:, pair, :, :], in0=pixels[:, pair, :, 1, :, 0], in1=pixels[:, pair, :, 1, :, 1], op=ALU.add
             )
+
+        def join_rows(c):
+            pair = slice(c, c + 2)
             nc.vector.tensor_tensor(
                 out=by_channel[:, pair, :, :], in0=by_channel[:, pair, :, :], in1=bottom[:, pair, :, :], op=ALU.subtract
             )
             nc.scalar.activation(out=squares[:, pair, :, :], in_=by_channel[:, pair, :, :], func=ACT.Square)
+
+        for c in range(0, CH, 2):
+            rows_of_blocks(c)
+            if c > 0:
+                join_rows(c - 2)
+            if c == 4:
+                regroup_w(PASS_ORDER[0], WIDE)
+                regroup_w(PASS_ORDER[0], REST)
+        join_rows(CH - 2)
         for r in range(BAND_ROWS):
-            nc.scalar.copy(
-                out=detail[:, r, PAD : PAD + DETAIL_W, :].rearrange("p j (h c) -> p h j c", h=2),
-                in_=by_channel[:, :, r, :].rearrange("p (h c) j -> p h j c", h=2),
-            )
+            sorted_row = detail[:, r, PAD : PAD + DETAIL_W, :].rearrange("p j (h c) -> p h j c", h=2)
+            row_by_channel = by_channel[:, :, r, :].rearrange("p (h c) j -> p h j c", h=2)
             cols = slice(r * ROW_LEN, (r + 1) * ROW_LEN)
-            nc.scalar.dma_start(out=scratch[BATCH : BATCH + P, cols], in_=detail[:, r, :, :].rearrange("p j c -> p (j c)"))
+            if r % 2 == 0:
+                nc.scalar.copy(out=sorted_row, in_=row_by_channel)
+                nc.scalar.dma_start(out=scratch[BATCH : BATCH + P, cols], in_=detail[:, r, :, :].rearrange("p j c -> p (j c)"))
+            else:
+                nc.vector.tensor_copy(out=sorted_row, in_=row_by_channel)
+                nc.sync.dma_start(out=scratch[BATCH : BATCH + P, cols], in_=detail[:, r, :, :].rearrange("p j c -> p (j c)"))
         for r in range(BAND_ROWS):
             cols = slice(r * ROW_LEN, (r + 1) * ROW_LEN)
             nc.sync.dma_start(out=detail_up[:, r, :, :].rearrange("p j c -> p (j c)"), in_=scratch[0:P, cols])
             nc.sync.dma_start(out=detail_dn[:, r, :, :].rearrange("p j c -> p (j c)"), in_=scratch[2 * BATCH : 2 * BATCH + P, cols])
-        for g in range(EARLY_W, PASSES):
-            nc.sync.dma_start(out=w_raws[g][:], in_=w_by_pass[g])
+        for g in PASS_ORDER[EARLY_W:]:
+            load_w(g)
 
-        strip_sums = keep.tile([P, 2, 18], F32)
-        nc.vector.memset(strip_sums[:], 0.0)
         nc.vector.tensor_reduce(
-            out=strip_sums[:, 0, 1:17],
-            in_=by_channel[:].rearrange("p c r (e l) -> p e (c r) l", l=PAD),
-            axis=AX.XY,
-            op=ALU.add,
+            out=strip_sums[:, 0, 1:17], in_=by_channel[:].rearrange("p c r (e l) -> p e (c r) l", l=PAD), axis=AX.XY, op=ALU.add
         )
         nc.vector.tensor_reduce(
-            out=strip_sums[:, 1, 1:17],
-            in_=squares[:].rearrange("p c r (e l) -> p e (c r) l", l=PAD),
-            axis=AX.XY,
-            op=ALU.add,
+            out=strip_sums[:, 1, 1:17], in_=squares[:].rearrange("p c r (e l) -> p e (c r) l", l=PAD), axis=AX.XY, op=ALU.add
         )
         window_sums = keep.tile([P, 2, 2, GRID], F32)
         inner = strip_sums[:, :, 1:17].rearrange("p q (j v) -> p q j v", v=2)
@@ -200,16 +254,14 @@ def tile_shiftedpatchtokenization_pb_kernel(tc, x, ln2_g, ln2_b, w2, b2, tok, ou
         nc.vector.tensor_tensor(out=window_sums[:, 0, :, :], in0=inner[:, :, :, 0], in1=inner[:, :, :, 1], op=ALU.add)
         nc.vector.tensor_tensor(out=window_sums[:, 1, :, :], in0=left[:, :, :, 0], in1=right[:, :, :, 1], op=ALU.add)
         nc.vector.tensor_tensor(out=window_sums[:, 1, :, :], in0=window_sums[:, 1, :, :], in1=window_sums[:, 0, :, :], op=ALU.add)
-        token_sums = small_psum.tile([P, 2 * GRID], F32, tag="small")
+        token_sums = turn_psum.tile([P, 2 * GRID], F32, tag="turned")
         nc.tensor.matmul(
             out=token_sums[:], lhsT=sum_own[:], rhs=window_sums[:, 0, :, :].rearrange("p q j -> p (q j)"), start=True, stop=False
         )
         nc.tensor.matmul(
             out=token_sums[:], lhsT=sum_near[:], rhs=window_sums[:, 1, :, :].rearrange("p q j -> p (q j)"), start=False, stop=True
         )
-        def add_bias(m):
-            nc.vector.tensor_tensor(out=tok_bias[:, m, :], in0=tok_in[:, m, :], in1=bias_all[:], op=ALU.add)
-
+        regroup_w(PASS_ORDER[1], WIDE)
         add_bias(0)
         mean = keep.tile([P, GRID], F32)
         mean_sq = keep.tile([P, GRID], F32)
@@ -233,37 +285,32 @@ def tile_shiftedpatchtokenization_pb_kernel(tc, x, ln2_g, ln2_b, w2, b2, tok, ou
         nc.vector.tensor_scalar(out=newton[:], in0=newton[:], scalar1=-0.5, scalar2=1.5, op0=ALU.mult, op1=ALU.add)
         nc.vector.tensor_tensor(out=rstd[:], in0=rstd0[:], in1=newton[:], op=ALU.mult)
         nc.vector.scalar_tensor_tensor(out=shift[:], in0=mean[:], scalar=-1.0, in1=rstd[:], op0=ALU.mult, op1=ALU.mult)
+        regroup_w(PASS_ORDER[1], REST)
+        regroup_w(PASS_ORDER[2], WIDE)
+        regroup_w(PASS_ORDER[2], REST)
+        quantise_w(PASS_ORDER[0])
         add_bias(2)
         add_bias(3)
+        quantise_w(PASS_ORDER[1])
 
-        w_codes = keep.tile([P, PASSES, DIM], U32, align_bytes=64)
-        w_scales = keep.tile([P, PASSES, DIM], U8, align_bytes=64)
-        for g in range(PASSES):
-            w_grp = w_grp_pool.tile([P, DIM, PACK], BF16, align_bytes=64)
-            for cols in (slice(0, N_WIDE), slice(N_WIDE, DIM)):
-                nc.scalar.copy(
-                    out=w_grp[:, cols, :].rearrange("p (n i) t -> p n t i", i=4),
-                    in_=w_raws[g][:, :, cols].rearrange("p t (n i) -> p n t i", i=4),
-                )
-                nc.vector.quantize_mx(
-                    out=w_codes[:, g, cols].bitcast(FP8X4),
-                    scales=w_scales[:, g, cols],
-                    in_=w_grp[:, cols, :].rearrange("p n t -> p (n t)"),
-                )
-
-        normed = keep.tile([P, GRID, HALF_K], F32)
+        normed = keep.tile([P, GRID, HALF_K], F32, tag="normed")
         normed_v = normed[:].rearrange("p j (r q s c) -> p j r q s c", r=BAND_ROWS, q=PATCH, s=VIEWS, c=CH)
         views = ((detail, 0), (detail_up, -PAD), (detail_up, PAD), (detail_dn, -PAD), (detail_dn, PAD))
         planes = keep.tile([P, SLOTS, J_GROUPS, GROUP_TOKENS], BF16, tag="image")
-        z_codes = keep.tile([P, PASSES, TOKENS], U32, align_bytes=64)
-        z_scales = keep.tile([P, PASSES, TOKENS], U8, align_bytes=64)
 
-        for jq in range(J_GROUPS):
-            toks = slice(jq * GROUP_TOKENS, (jq + 1) * GROUP_TOKENS)
+        def normalise(jq, s):
+            source, dx = views[s]
             for j in range(jq * J_GROUP, (jq + 1) * J_GROUP):
-                for s in range(VIEWS):
-                    source, dx = views[s]
-                    first = PAD + PATCH * j + dx
+                first = PAD + PATCH * j + dx
+                if s == 0:
+                    nc.scalar.activation(
+                        out=normed_v[:, j, :, :, s, :],
+                        in_=source[:, :, first : first + PATCH, :],
+                        func=ACT.Identity,
+                        scale=rstd[:, j : j + 1],
+                        bias=shift[:, j : j + 1],
+                    )
+                else:
                     nc.vector.tensor_scalar(
                         out=normed_v[:, j, :, :, s, :],
                         in0=source[:, :, first : first + PATCH, :],
@@ -272,49 +319,99 @@ def tile_shiftedpatchtokenization_pb_kernel(tc, x, ln2_g, ln2_b, w2, b2, tok, ou
                         op0=ALU.mult,
                         op1=ALU.add,
                     )
-            for sg in range(HALF_SLOTS):
-                turned = turn_psum.tile([P, J_GROUP, P], F32)
-                for j4 in range(J_GROUP):
-                    nc.tensor.transpose(
-                        out=turned[:, j4, :],
-                        in_=normed[:, jq * J_GROUP + j4, sg * P : (sg + 1) * P],
-                        identity=turn_order[:],
-                    )
-                for h in range(2):
-                    slot = sg + HALF_SLOTS * h
-                    nc.scalar.activation(
-                        out=planes[:, slot, jq, :].rearrange("p (g j) -> p g j", j=J_GROUP),
-                        in_=turned[:, :, 64 * h : 64 * h + 64].rearrange("p j g -> p g j"),
-                        func=ACT.Identity,
-                        scale=gain_t[:, slot : slot + 1],
-                        bias=gain_t[:, 32 + slot : 33 + slot],
-                    )
-                for g in range(PASSES):
-                    if max([(PACK * g + t) % HALF_SLOTS for t in range(PACK)]) == sg:
-                        z_grp = z_grp_pool.tile([P, GROUP_TOKENS, PACK], BF16, align_bytes=64)
-                        nc.vector.tensor_copy(
-                            out=z_grp[:].rearrange("p (w i) t -> p w t i", i=4),
-                            in_=planes[:, PACK * g : PACK * (g + 1), jq, :].rearrange("p t (w i) -> p w t i", i=4),
-                        )
-                        nc.vector.quantize_mx(
-                            out=z_codes[:, g, toks].bitcast(FP8X4),
-                            scales=z_scales[:, g, toks],
-                            in_=z_grp[:].rearrange("p w t -> p (w t)"),
-                        )
-            for m in (2 * jq, 2 * jq + 1):
+
+        turned_tiles = {}
+
+        def turn(n):
+            jq, sg = divmod(n, HALF_SLOTS)
+            turned = turn_psum.tile([P, J_GROUP, P], F32)
+            turned_tiles[n] = turned
+            for j4 in range(J_GROUP):
+                nc.tensor.transpose(
+                    out=turned[:, j4, :], in_=normed[:, jq * J_GROUP + j4, sg * P : (sg + 1) * P], identity=turn_order[:]
+                )
+
+        def empty(n):
+            jq, sg = divmod(n, HALF_SLOTS)
+            for h in range(2):
+                slot = sg + HALF_SLOTS * h
+                nc.scalar.activation(
+                    out=planes[:, slot, jq, :].rearrange("p (g j) -> p g j", j=J_GROUP),
+                    in_=turned_tiles[n][:, :, 64 * h : 64 * h + 64].rearrange("p j g -> p g j"),
+                    func=ACT.Identity,
+                    scale=gain_t[:, slot : slot + 1],
+                    bias=gain_t[:, 32 + slot : 33 + slot],
+                )
+
+        z_grps = {}
+
+        def regroup_z(jq, g):
+            z_grp = z_grp_pool.tile([P, GROUP_TOKENS, PACK], BF16, align_bytes=64)
+            z_grps[(jq, g)] = z_grp
+            nc.vector.tensor_copy(
+                out=z_grp[:].rearrange("p (w i) t -> p w t i", i=4),
+                in_=planes[:, PACK * g : PACK * (g + 1), jq, :].rearrange("p t (w i) -> p w t i", i=4),
+            )
+
+        def quantise_z(jq, g):
+            toks = slice(jq * GROUP_TOKENS, (jq + 1) * GROUP_TOKENS)
+            nc.vector.quantize_mx(
+                out=z_codes[:, g, toks].bitcast(FP8X4),
+                scales=z_scales[:, g, toks],
+                in_=z_grps[(jq, g)][:].rearrange("p w t -> p (w t)"),
+            )
+
+        def passes_done_at(n):
+            return [(n // HALF_SLOTS, g) for g in PASS_ORDER if 0 <= n < STEPS and LAST_PLANE[g] == n % HALF_SLOTS]
+
+        accs = {}
+
+        def multiply(jq, g):
+            for bh in range(2):
+                m = 2 * jq + bh
                 rows = slice(m * P, (m + 1) * P)
-                acc_wide = wide_psum.tile([P, N_WIDE], F32)
-                acc_rest = rest_psum.tile([P, DIM - N_WIDE], F32)
-                for acc, cols in ((acc_wide, slice(0, N_WIDE)), (acc_rest, slice(N_WIDE, DIM))):
-                    for g in range(PASSES):
-                        nc.tensor.matmul_mx(
-                            out=acc[:],
-                            lhsT=z_codes[:, g, rows].bitcast(FP8X4),
-                            lhsT_scale=z_scales[:, g, rows],
-                            rhs=w_codes[:, g, cols].bitcast(FP8X4),
-                            rhs_scale=w_scales[:, g, cols],
-                            start=(g == 0),
-                            stop=(g == PASSES - 1),
-                        )
-                    nc.vector.tensor_tensor(out=tok_bias[:, m, cols], in0=acc[:], in1=tok_bias[:, m, cols], op=ALU.add)
-                nc.sync.dma_start(out=token_rows(out, m), in_=tok_bias[:, m, :])
+                if g == PASS_ORDER[0]:
+                    acc_wide = acc_psum.tile([P, N_WIDE], F32, tag="wide%d" % bh)
+                    acc_rest = acc_psum.tile([P, DIM - N_WIDE], F32, tag="rest%d" % bh)
+                    accs[m] = ((acc_wide, WIDE), (acc_rest, REST))
+                for acc, cols in accs[m]:
+                    nc.tensor.matmul_mx(
+                        out=acc[:],
+                        lhsT=z_codes[:, g, rows].bitcast(FP8X4),
+                        lhsT_scale=z_scales[:, g, rows],
+                        rhs=w_codes[:, g, cols].bitcast(FP8X4),
+                        rhs_scale=w_scales[:, g, cols],
+                        start=(g == PASS_ORDER[0]),
+                        stop=(g == PASS_ORDER[-1]),
+                    )
+                if g == PASS_ORDER[-1]:
+                    for acc, cols in accs[m]:
+                        nc.vector.tensor_tensor(out=tok_bias[:, m, cols], in0=acc[:], in1=tok_bias[:, m, cols], op=ALU.add)
+                    nc.sync.dma_start(out=token_rows(out, m), in_=tok_bias[:, m, :])
+
+        normalise(0, 0)
+        normalise(1, 0)
+        regroup_w(PASS_ORDER[3], WIDE)
+        regroup_w(PASS_ORDER[3], REST)
+        quantise_w(PASS_ORDER[2])
+        for jq in range(J_GROUPS):
+            for s in range(1, VIEWS):
+                normalise(jq, s)
+        quantise_w(PASS_ORDER[3])
+        for n in range(AHEAD):
+            turn(n)
+        for n in range(STEPS + LAG):
+            if n + AHEAD < STEPS:
+                turn(n + AHEAD)
+            if n < STEPS:
+                empty(n)
+            for jq, g in passes_done_at(n):
+                regroup_z(jq, g)
+            for jq, g in passes_done_at(n - 1):
+                quantise_z(jq, g)
+            if n == LAST_W_STEP:
+                regroup_w(PASS_ORDER[4], WIDE)
+                regroup_w(PASS_ORDER[4], REST)
+                quantise_w(PASS_ORDER[4])
+            for jq, g in passes_done_at(n - LAG):
+                multiply(jq, g)

@@ -45,8 +45,9 @@ STEPS = J_GROUPS * HALF_SLOTS
 TURN_BANKS = 4
 AHEAD = TURN_BANKS - 1
 LAG = 6
-LAST_W_STEP = 6
-EARLY_W = 4
+SCALAR_W = 3
+W_STEP = 4
+EARLY_W = 2
 HAAR_SCALE = 6.0
 EPS = 1e-5 * HAAR_SCALE * HAAR_SCALE
 
@@ -108,14 +109,11 @@ def tile_shiftedpatchtokenization_pb_kernel(tc, x, ln2_g, ln2_b, w2, b2, tok, ou
         nc.scalar.dma_start(out=bias_row[0:1, :], in_=b2.unsqueeze(0))
         nc.scalar.dma_start(out=scratch[0:BATCH, :], in_=zero_rows[:])
         nc.scalar.dma_start(out=scratch[P + BATCH : P + 2 * BATCH, :], in_=zero_rows[:])
-        for c in range(4):
-            load_image(c)
-        load_w(PASS_ORDER[0])
-        for c in range(4, CH):
+        for c in range(CH):
             load_image(c)
         for m in range(4):
             nc.sync.dma_start(out=tok_in[:, m, :], in_=token_rows(tok, m))
-        for g in PASS_ORDER[1:EARLY_W]:
+        for g in PASS_ORDER[0:EARLY_W]:
             load_w(g)
 
         nc.scalar.activation(out=one_root[:], in_=one[:], func=ACT.Sqrt)
@@ -125,6 +123,8 @@ def tile_shiftedpatchtokenization_pb_kernel(tc, x, ln2_g, ln2_b, w2, b2, tok, ou
         nc.gpsimd.memset(detail[:, :, 0:PAD, :], 0.0)
         nc.gpsimd.memset(detail[:, :, PAD + DETAIL_W : PADDED_W, :], 0.0)
 
+        ident_bf = keep.tile([P, P], BF16)
+        nc.vector.tensor_copy(out=ident_bf[:], in_=ident[:])
         ident_ihb = ident[:].rearrange("p (i h b) -> p i h b", i=GRID, h=2)
         turn_order = keep.tile([P, P], F32)
         nc.vector.tensor_copy(
@@ -166,9 +166,11 @@ def tile_shiftedpatchtokenization_pb_kernel(tc, x, ln2_g, ln2_b, w2, b2, tok, ou
         nc.tensor.matmul(out=bias_wide[:], lhsT=ones[:], rhs=bias_row[:, 0:N_WIDE], start=True, stop=True)
         nc.tensor.matmul(out=bias_rest[:], lhsT=ones[:], rhs=bias_row[:, N_WIDE:DIM], start=True, stop=True)
 
-        def add_bias(m):
-            nc.vector.tensor_tensor(out=tok_bias[:, m, 0:N_WIDE], in0=bias_wide[:], in1=tok_in[:, m, 0:N_WIDE], op=ALU.add)
-            nc.vector.tensor_tensor(out=tok_bias[:, m, N_WIDE:DIM], in0=bias_rest[:], in1=tok_in[:, m, N_WIDE:DIM], op=ALU.add)
+        bias_all = keep.tile([P, DIM], BF16)
+        nc.scalar.copy(out=bias_all[:, WIDE], in_=bias_wide[:])
+        nc.scalar.copy(out=bias_all[:, REST], in_=bias_rest[:])
+        for m in range(4):
+            nc.gpsimd.tensor_tensor(out=tok_bias[:, m, :], in0=tok_in[:, m, :], in1=bias_all[:], op=ALU.add)
 
         w_grps = {}
 
@@ -178,7 +180,7 @@ def tile_shiftedpatchtokenization_pb_kernel(tc, x, ln2_g, ln2_b, w2, b2, tok, ou
                 w_grps[g] = w_grp
             grouped = w_grps[g][:, cols, :].rearrange("p (n i) t -> p n t i", i=4)
             rows = w_raws[g][:, :, cols].rearrange("p t (n i) -> p n t i", i=4)
-            if g == PASS_ORDER[-1]:
+            if g in PASS_ORDER[SCALAR_W:]:
                 nc.vector.tensor_copy(out=grouped, in_=rows)
             else:
                 nc.scalar.copy(out=grouped, in_=rows)
@@ -193,10 +195,21 @@ def tile_shiftedpatchtokenization_pb_kernel(tc, x, ln2_g, ln2_b, w2, b2, tok, ou
 
         pixels = image[:].rearrange("p c (r u j v) -> p c r u j v", r=BAND_ROWS, u=2, j=DETAIL_W, v=2)
         by_channel = keep.tile([P, CH, BAND_ROWS, DETAIL_W], F32)
-        bottom = keep.tile([P, CH, BAND_ROWS, DETAIL_W], F32)
         squares = keep.tile([P, CH, BAND_ROWS, DETAIL_W], F32)
+        bottoms = {}
+
         def rows_of_blocks(c):
             pair = slice(c, c + 2)
+            bottom = turn_psum.tile([P, 2, BAND_ROWS, DETAIL_W], F32, tag="turned")
+            bottoms[c] = bottom
+            for v in range(2):
+                nc.tensor.matmul(
+                    out=bottom[:].rearrange("p c r j -> p (c r) j"),
+                    lhsT=ident_bf[:],
+                    rhs=pixels[:, pair, :, 1, :, v].rearrange("p c r j -> p (c r) j"),
+                    start=(v == 0),
+                    stop=(v == 1),
+                )
             nc.vector.scalar_tensor_tensor(
                 out=by_channel[:, pair, :, :],
                 in0=pixels[:, pair, :, 0, :, 0],
@@ -205,24 +218,16 @@ def tile_shiftedpatchtokenization_pb_kernel(tc, x, ln2_g, ln2_b, w2, b2, tok, ou
                 op0=ALU.mult,
                 op1=ALU.subtract,
             )
-            nc.vector.tensor_tensor(
-                out=bottom[:, pair, :, :], in0=pixels[:, pair, :, 1, :, 0], in1=pixels[:, pair, :, 1, :, 1], op=ALU.add
-            )
 
         def join_rows(c):
             pair = slice(c, c + 2)
-            nc.vector.tensor_tensor(
-                out=by_channel[:, pair, :, :], in0=by_channel[:, pair, :, :], in1=bottom[:, pair, :, :], op=ALU.subtract
-            )
+            nc.vector.tensor_tensor(out=by_channel[:, pair, :, :], in0=by_channel[:, pair, :, :], in1=bottoms[c][:], op=ALU.subtract)
             nc.scalar.activation(out=squares[:, pair, :, :], in_=by_channel[:, pair, :, :], func=ACT.Square)
 
         for c in range(0, CH, 2):
             rows_of_blocks(c)
             if c > 0:
                 join_rows(c - 2)
-            if c == 4:
-                regroup_w(PASS_ORDER[0], WIDE)
-                regroup_w(PASS_ORDER[0], REST)
         join_rows(CH - 2)
         for r in range(BAND_ROWS):
             sorted_row = detail[:, r, PAD : PAD + DETAIL_W, :].rearrange("p j (h c) -> p h j c", h=2)
@@ -261,8 +266,8 @@ def tile_shiftedpatchtokenization_pb_kernel(tc, x, ln2_g, ln2_b, w2, b2, tok, ou
         nc.tensor.matmul(
             out=token_sums[:], lhsT=sum_near[:], rhs=window_sums[:, 1, :, :].rearrange("p q j -> p (q j)"), start=False, stop=True
         )
-        regroup_w(PASS_ORDER[1], WIDE)
-        add_bias(0)
+        regroup_w(PASS_ORDER[0], WIDE)
+        regroup_w(PASS_ORDER[0], REST)
         mean = keep.tile([P, GRID], F32)
         mean_sq = keep.tile([P, GRID], F32)
         var = keep.tile([P, GRID], F32)
@@ -272,25 +277,19 @@ def tile_shiftedpatchtokenization_pb_kernel(tc, x, ln2_g, ln2_b, w2, b2, tok, ou
         rstd = keep.tile([P, GRID], F32)
         shift = keep.tile([P, GRID], F32)
         nc.vector.tensor_scalar(out=mean[:], in0=token_sums[:, 0:GRID], scalar1=1.0 / K, scalar2=None, op0=ALU.mult)
+        nc.vector.tensor_scalar(out=var[:], in0=token_sums[:, GRID : 2 * GRID], scalar1=1.0 / K, scalar2=EPS, op0=ALU.mult, op1=ALU.add)
         nc.vector.tensor_tensor(out=mean_sq[:], in0=mean[:], in1=mean[:], op=ALU.mult)
-        nc.vector.scalar_tensor_tensor(
-            out=var[:], in0=token_sums[:, GRID : 2 * GRID], scalar=1.0 / K, in1=mean_sq[:], op0=ALU.mult, op1=ALU.subtract
-        )
-        nc.vector.tensor_scalar(out=var[:], in0=var[:], scalar1=EPS, scalar2=None, op0=ALU.add)
+        nc.vector.tensor_tensor(out=var[:], in0=var[:], in1=mean_sq[:], op=ALU.subtract)
         nc.scalar.activation(out=std[:], in_=var[:], func=ACT.Sqrt)
-        add_bias(1)
         nc.vector.reciprocal(out=rstd0[:], in_=std[:])
         nc.vector.tensor_tensor(out=newton[:], in0=var[:], in1=rstd0[:], op=ALU.mult)
         nc.vector.tensor_tensor(out=newton[:], in0=newton[:], in1=rstd0[:], op=ALU.mult)
         nc.vector.tensor_scalar(out=newton[:], in0=newton[:], scalar1=-0.5, scalar2=1.5, op0=ALU.mult, op1=ALU.add)
         nc.vector.tensor_tensor(out=rstd[:], in0=rstd0[:], in1=newton[:], op=ALU.mult)
         nc.vector.scalar_tensor_tensor(out=shift[:], in0=mean[:], scalar=-1.0, in1=rstd[:], op0=ALU.mult, op1=ALU.mult)
+        regroup_w(PASS_ORDER[1], WIDE)
         regroup_w(PASS_ORDER[1], REST)
-        regroup_w(PASS_ORDER[2], WIDE)
-        regroup_w(PASS_ORDER[2], REST)
         quantise_w(PASS_ORDER[0])
-        add_bias(2)
-        add_bias(3)
         quantise_w(PASS_ORDER[1])
 
         normed = keep.tile([P, GRID, HALF_K], F32, tag="normed")
@@ -391,12 +390,11 @@ def tile_shiftedpatchtokenization_pb_kernel(tc, x, ln2_g, ln2_b, w2, b2, tok, ou
 
         normalise(0, 0)
         normalise(1, 0)
-        regroup_w(PASS_ORDER[3], WIDE)
-        regroup_w(PASS_ORDER[3], REST)
-        quantise_w(PASS_ORDER[2])
         for jq in range(J_GROUPS):
             for s in range(1, VIEWS):
                 normalise(jq, s)
+        regroup_w(PASS_ORDER[3], WIDE)
+        regroup_w(PASS_ORDER[3], REST)
         quantise_w(PASS_ORDER[3])
         for n in range(AHEAD):
             turn(n)
@@ -409,7 +407,11 @@ def tile_shiftedpatchtokenization_pb_kernel(tc, x, ln2_g, ln2_b, w2, b2, tok, ou
                 regroup_z(jq, g)
             for jq, g in passes_done_at(n - 1):
                 quantise_z(jq, g)
-            if n == LAST_W_STEP:
+            if n == W_STEP:
+                regroup_w(PASS_ORDER[2], WIDE)
+                regroup_w(PASS_ORDER[2], REST)
+            if n == W_STEP + 2:
+                quantise_w(PASS_ORDER[2])
                 regroup_w(PASS_ORDER[4], WIDE)
                 regroup_w(PASS_ORDER[4], REST)
                 quantise_w(PASS_ORDER[4])

@@ -20,8 +20,6 @@ BAND_ROWS = 4
 DETAIL_W = 64
 PAD = 4
 PADDED_W = DETAIL_W + 2 * PAD
-ROW_LEN = PADDED_W * CH
-BAND_LEN = BAND_ROWS * ROW_LEN
 GRID = 8
 PATCH = 8
 VIEWS = 5
@@ -80,7 +78,6 @@ def tile_shiftedpatchtokenization_pb_kernel(tc, x, ln2_g, ln2_b, w2, b2, tok, ou
         detail = keep.tile([P, BAND_ROWS, PADDED_W, CH], F32)
         detail_up = keep.tile([P, BAND_ROWS, PADDED_W, CH], F32)
         detail_dn = keep.tile([P, BAND_ROWS, PADDED_W, CH], F32)
-        scratch = out.rearrange("b n d -> (b n d)")[0 : (P + 2 * BATCH) * BAND_LEN].rearrange("(q f) -> q f", f=BAND_LEN)
 
         def token_rows(dram, m):
             jq, bh = divmod(m, 2)
@@ -98,17 +95,13 @@ def tile_shiftedpatchtokenization_pb_kernel(tc, x, ln2_g, ln2_b, w2, b2, tok, ou
         ones = keep.tile([P, P], BF16)
         one = keep.tile([P, 1], F32)
         one_root = keep.tile([P, 1], F32)
-        zero_rows = keep.tile([BATCH, BAND_LEN], F32, tag="normed")
         nc.vector.memset(gain_rows[:], 0.0)
-        nc.vector.memset(zero_rows[:], 0.0)
         nc.vector.memset(bias_row[:], 0.0)
         nc.vector.memset(ones[:], 1.0)
         nc.vector.memset(one[:], 1.0)
         nc.scalar.dma_start(out=gain_rows[0:SLOTS, :], in_=ln2_g.rearrange("(s p) -> s p", p=P))
         nc.scalar.dma_start(out=gain_rows[32 : 32 + SLOTS, :], in_=ln2_b.rearrange("(s p) -> s p", p=P))
         nc.scalar.dma_start(out=bias_row[0:1, :], in_=b2.unsqueeze(0))
-        nc.scalar.dma_start(out=scratch[0:BATCH, :], in_=zero_rows[:])
-        nc.scalar.dma_start(out=scratch[P + BATCH : P + 2 * BATCH, :], in_=zero_rows[:])
         for c in range(CH):
             load_image(c)
         for m in range(4):
@@ -120,8 +113,11 @@ def tile_shiftedpatchtokenization_pb_kernel(tc, x, ln2_g, ln2_b, w2, b2, tok, ou
 
         ident = keep.tile([P, P], F32)
         make_identity(nc, ident[:])
-        nc.gpsimd.memset(detail[:, :, 0:PAD, :], 0.0)
-        nc.gpsimd.memset(detail[:, :, PAD + DETAIL_W : PADDED_W, :], 0.0)
+        for band in (detail, detail_up, detail_dn):
+            nc.gpsimd.memset(band[:, :, 0:PAD, :], 0.0)
+            nc.gpsimd.memset(band[:, :, PAD + DETAIL_W : PADDED_W, :], 0.0)
+        nc.gpsimd.memset(detail_up[0:BATCH, :, :, :], 0.0)
+        nc.gpsimd.memset(detail_dn[96:P, :, :, :], 0.0)
 
         ident_bf = keep.tile([P, P], BF16)
         nc.vector.tensor_copy(out=ident_bf[:], in_=ident[:])
@@ -229,20 +225,18 @@ def tile_shiftedpatchtokenization_pb_kernel(tc, x, ln2_g, ln2_b, w2, b2, tok, ou
             if c > 0:
                 join_rows(c - 2)
         join_rows(CH - 2)
+        def inner(band, rows, r):
+            return band[rows, r, PAD : PAD + DETAIL_W, :].rearrange("p j c -> p (j c)")
+
         for r in range(BAND_ROWS):
             sorted_row = detail[:, r, PAD : PAD + DETAIL_W, :].rearrange("p j (h c) -> p h j c", h=2)
             row_by_channel = by_channel[:, :, r, :].rearrange("p (h c) j -> p h j c", h=2)
-            cols = slice(r * ROW_LEN, (r + 1) * ROW_LEN)
             if r % 2 == 0:
                 nc.scalar.copy(out=sorted_row, in_=row_by_channel)
-                nc.scalar.dma_start(out=scratch[BATCH : BATCH + P, cols], in_=detail[:, r, :, :].rearrange("p j c -> p (j c)"))
             else:
                 nc.vector.tensor_copy(out=sorted_row, in_=row_by_channel)
-                nc.sync.dma_start(out=scratch[BATCH : BATCH + P, cols], in_=detail[:, r, :, :].rearrange("p j c -> p (j c)"))
-        for r in range(BAND_ROWS):
-            cols = slice(r * ROW_LEN, (r + 1) * ROW_LEN)
-            nc.sync.dma_start(out=detail_up[:, r, :, :].rearrange("p j c -> p (j c)"), in_=scratch[0:P, cols])
-            nc.sync.dma_start(out=detail_dn[:, r, :, :].rearrange("p j c -> p (j c)"), in_=scratch[2 * BATCH : 2 * BATCH + P, cols])
+            nc.sync.dma_start(out=inner(detail_up, slice(BATCH, P), r), in_=inner(detail, slice(0, P - BATCH), r))
+            nc.sync.dma_start(out=inner(detail_dn, slice(0, P - BATCH), r), in_=inner(detail, slice(BATCH, P), r))
         for g in PASS_ORDER[EARLY_W:]:
             load_w(g)
 
@@ -292,7 +286,7 @@ def tile_shiftedpatchtokenization_pb_kernel(tc, x, ln2_g, ln2_b, w2, b2, tok, ou
         quantise_w(PASS_ORDER[0])
         quantise_w(PASS_ORDER[1])
 
-        normed = keep.tile([P, GRID, HALF_K], F32, tag="normed")
+        normed = keep.tile([P, GRID, HALF_K], F32)
         normed_v = normed[:].rearrange("p j (r q s c) -> p j r q s c", r=BAND_ROWS, q=PATCH, s=VIEWS, c=CH)
         views = ((detail, 0), (detail_up, -PAD), (detail_up, PAD), (detail_dn, -PAD), (detail_dn, PAD))
         planes = keep.tile([P, SLOTS, J_GROUPS, GROUP_TOKENS], BF16, tag="image")
@@ -386,7 +380,7 @@ def tile_shiftedpatchtokenization_pb_kernel(tc, x, ln2_g, ln2_b, w2, b2, tok, ou
                 if g == PASS_ORDER[-1]:
                     for acc, cols in accs[m]:
                         nc.vector.tensor_tensor(out=tok_bias[:, m, cols], in0=acc[:], in1=tok_bias[:, m, cols], op=ALU.add)
-                    nc.sync.dma_start(out=token_rows(out, m), in_=tok_bias[:, m, :])
+                        nc.sync.dma_start(out=token_rows(out, m)[:, :, cols], in_=tok_bias[:, m, cols])
 
         normalise(0, 0)
         normalise(1, 0)

from contextlib import ExitStack

import concourse.mybir as mybir
from concourse.masks import make_identity

F32 = mybir.dt.float32
BF16 = mybir.dt.bfloat16
U32 = mybir.dt.uint32
U8 = mybir.dt.uint8
FP8X4 = mybir.dt.float8_e4m3fn_x4
ALU = mybir.AluOpType
ACT = mybir.ActivationFunctionType
AX = mybir.AxisListType

P = 128
BATCH = 8
CH = 8
BANDS = 16
BAND_ROWS = 4
DETAIL_W = 64
PAD = 4
PADDED_W = DETAIL_W + 2 * PAD
GRID = 8
PATCH = 8
VIEWS = 5
HALF_K = BAND_ROWS * PATCH * VIEWS * CH
K = 2 * HALF_K
DIM = 768
TOKENS = BATCH * GRID * GRID
SLOTS = K // P
PACK = 4
PASSES = SLOTS // PACK
HALF_SLOTS = HALF_K // P
J_GROUP = 4
J_GROUPS = GRID // J_GROUP
GROUP_TOKENS = TOKENS // J_GROUPS
N_WIDE = 512
WIDE = slice(0, N_WIDE)
REST = slice(N_WIDE, DIM)
LAST_PLANE = [max([(PACK * g + t) % HALF_SLOTS for t in range(PACK)]) for g in range(PASSES)]
PASS_ORDER = sorted(range(PASSES), key=lambda g: LAST_PLANE[g])
STEPS = J_GROUPS * HALF_SLOTS
TURN_BANKS = 4
AHEAD = TURN_BANKS - 1
LAG = 6
SCALAR_W = 3
W_STEP = 4
EARLY_W = 2
HAAR_SCALE = 6.0
EPS = 1e-5 * HAAR_SCALE * HAAR_SCALE

FLOPS = 2 * TOKENS * K * DIM


def tile_shiftedpatchtokenization_pb_kernel(tc, x, ln2_g, ln2_b, w2, b2, tok, out):
    nc = tc.nc
    with ExitStack() as ctx:
        keep = ctx.enter_context(tc.tile_pool(name="keep", bufs=1))
        w_raw_pool = ctx.enter_context(tc.tile_pool(name="w_raw", bufs=PASSES))
        w_grp_pool = ctx.enter_context(tc.tile_pool(name="w_grp", bufs=3))
        z_grp_pool = ctx.enter_context(tc.tile_pool(name="z_grp", bufs=3))
        turn_psum = ctx.enter_context(tc.psum_pool(name="turn_psum", bufs=TURN_BANKS))
        acc_psum = ctx.enter_context(tc.psum_pool(name="acc_psum", bufs=1))
        ctx.enter_context(tc.manual_schedule())

        image = keep.tile([P, CH, 8 * 128], BF16, tag="image")
        w_raws = []
        for g in range(PASSES):
            w_raw = w_raw_pool.tile([P, PACK, DIM], BF16)
            w_raws.append(w_raw)
        w_by_pass = w2.rearrange("(g t p) n -> g p t n", t=PACK, p=P)
        w_codes = keep.tile([P, PASSES, DIM], U32, align_bytes=64)
        w_scales = keep.tile([P, PASSES, DIM], U8, align_bytes=64)
        z_codes = keep.tile([P, PASSES, TOKENS], U32, align_bytes=64)
        z_scales = keep.tile([P, PASSES, TOKENS], U8, align_bytes=64)
        tok_in = keep.tile([P, 4, DIM], BF16)
        tok_bias = keep.tile([P, 4, DIM], F32)
        detail = keep.tile([P, BAND_ROWS, PADDED_W, CH], F32)
        detail_up = keep.tile([P, BAND_ROWS, PADDED_W, CH], F32)
        detail_dn = keep.tile([P, BAND_ROWS, PADDED_W, CH], F32)

        def token_rows(dram, m):
            jq, bh = divmod(m, 2)
            rows = dram[4 * bh : 4 * bh + 4, :, :]
            return rows.rearrange("b (i q j) d -> q (b i) j d", q=J_GROUPS, j=J_GROUP)[jq]

        def load_image(c):
            nc.sync.dma_start(out=image[:, c, :], in_=x[:, c, :, :].rearrange("b (a r) w -> a b (r w)", a=BANDS))

        def load_w(g):
            nc.sync.dma_start(out=w_raws[g][:], in_=w_by_pass[g])

        gain_rows = keep.tile([P, P], BF16)
        bias_row = keep.tile([P, DIM], BF16)
        ones = keep.tile([P, P], BF16)
        one = keep.tile([P, 1], F32)
        one_root = keep.tile([P, 1], F32)
        nc.vector.memset(gain_rows[:], 0.0)
        nc.vector.memset(bias_row[:], 0.0)
        nc.vector.memset(ones[:], 1.0)
        nc.vector.memset(one[:], 1.0)
        nc.scalar.dma_start(out=gain_rows[0:SLOTS, :], in_=ln2_g.rearrange("(s p) -> s p", p=P))
        nc.scalar.dma_start(out=gain_rows[32 : 32 + SLOTS, :], in_=ln2_b.rearrange("(s p) -> s p", p=P))
        nc.scalar.dma_start(out=bias_row[0:1, :], in_=b2.unsqueeze(0))
        for c in range(CH):
            load_image(c)
        for m in range(4):
            nc.sync.dma_start(out=tok_in[:, m, :], in_=token_rows(tok, m))
        for g in PASS_ORDER[0:EARLY_W]:
            load_w(g)

        nc.scalar.activation(out=one_root[:], in_=one[:], func=ACT.Sqrt)

        ident = keep.tile([P, P], F32)
        make_identity(nc, ident[:])
        for band in (detail, detail_up, detail_dn):
            nc.gpsimd.memset(band[:, :, 0:PAD, :], 0.0)
            nc.gpsimd.memset(band[:, :, PAD + DETAIL_W : PADDED_W, :], 0.0)
        nc.gpsimd.memset(detail_up[0:BATCH, :, :, :], 0.0)
        nc.gpsimd.memset(detail_dn[96:P, :, :, :], 0.0)

        ident_bf = keep.tile([P, P], BF16)
        nc.vector.tensor_copy(out=ident_bf[:], in_=ident[:])
        ident_ihb = ident[:].rearrange("p (i h b) -> p i h b", i=GRID, h=2)
        turn_order = keep.tile([P, P], F32)
        nc.vector.tensor_copy(
            out=turn_order[:].rearrange("p (h b i) -> p h b i", h=2, b=BATCH),
            in_=ident[:].rearrange("p (i h b) -> p h b i", i=GRID, h=2),
        )
        own_bands = keep.tile([P, GRID, BATCH], F32)
        near_bands = keep.tile([P, GRID, BATCH], F32)
        nc.vector.tensor_tensor(out=own_bands[:], in0=ident_ihb[:, :, 0, :], in1=ident_ihb[:, :, 1, :], op=ALU.add)
        nc.vector.tensor_copy(out=near_bands[:, 0:1, :], in_=own_bands[:, 0:1, :])
        nc.vector.tensor_tensor(
            out=near_bands[:, 1:GRID, :], in0=own_bands[:, 1:GRID, :], in1=ident_ihb[:, 0 : GRID - 1, 1, :], op=ALU.add
        )
        nc.vector.tensor_tensor(
            out=near_bands[:, 0 : GRID - 1, :], in0=near_bands[:, 0 : GRID - 1, :], in1=ident_ihb[:, 1:GRID, 0, :], op=ALU.add
        )
        sum_own = keep.tile([P, P], F32)
        sum_near = keep.tile([P, P], F32)
        nc.vector.tensor_copy(
            out=sum_own[:].rearrange("p (i h b) -> p i h b", i=GRID, h=2),
            in_=own_bands[:].unsqueeze(2).to_broadcast([P, GRID, 2, BATCH]),
        )
        nc.vector.tensor_copy(
            out=sum_near[:].rearrange("p (i h b) -> p i h b", i=GRID, h=2),
            in_=near_bands[:].unsqueeze(2).to_broadcast([P, GRID, 2, BATCH]),
        )
        strip_sums = keep.tile([P, 2, 18], F32)
        nc.vector.memset(strip_sums[:], 0.0)

        gain_f32 = keep.tile([P, P], F32)
        nc.vector.tensor_copy(out=gain_f32[:], in_=gain_rows[:])
        gain_ps = turn_psum.tile([P, P], F32, tag="turned")
        nc.tensor.transpose(out=gain_ps[:], in_=gain_f32[:], identity=ident[:])
        gain_t = keep.tile([P, P], F32)
        nc.vector.tensor_copy(out=gain_t[:], in_=gain_ps[:])

        bias_wide = acc_psum.tile([P, N_WIDE], F32, tag="wide0")
        bias_rest = acc_psum.tile([P, DIM - N_WIDE], F32, tag="rest0")
        nc.tensor.matmul(out=bias_wide[:], lhsT=ones[:], rhs=bias_row[:, 0:N_WIDE], start=True, stop=True)
        nc.tensor.matmul(out=bias_rest[:], lhsT=ones[:], rhs=bias_row[:, N_WIDE:DIM], start=True, stop=True)

        bias_all = keep.tile([P, DIM], BF16)
        nc.scalar.copy(out=bias_all[:, WIDE], in_=bias_wide[:])
        nc.scalar.copy(out=bias_all[:, REST], in_=bias_rest[:])
        for m in range(4):
            nc.gpsimd.tensor_tensor(out=tok_bias[:, m, :], in0=tok_in[:, m, :], in1=bias_all[:], op=ALU.add)

        w_grps = {}

        def regroup_w(g, cols):
            if g not in w_grps:
                w_grp = w_grp_pool.tile([P, DIM, PACK], BF16, align_bytes=64)
                w_grps[g] = w_grp
            grouped = w_grps[g][:, cols, :].rearrange("p (n i) t -> p n t i", i=4)
            rows = w_raws[g][:, :, cols].rearrange("p t (n i) -> p n t i", i=4)
            if g in PASS_ORDER[SCALAR_W:]:
                nc.vector.tensor_copy(out=grouped, in_=rows)
            else:
                nc.scalar.copy(out=grouped, in_=rows)

        def quantise_w(g):
            for cols in (WIDE, REST):
                nc.vector.quantize_mx(
                    out=w_codes[:, g, cols].bitcast(FP8X4),
                    scales=w_scales[:, g, cols],
                    in_=w_grps[g][:, cols, :].rearrange("p n t -> p (n t)"),
                )

        pixels = image[:].rearrange("p c (r u j v) -> p c r u j v", r=BAND_ROWS, u=2, j=DETAIL_W, v=2)
        by_channel = keep.tile([P, CH, BAND_ROWS, DETAIL_W], F32)
        squares = keep.tile([P, CH, BAND_ROWS, DETAIL_W], F32)
        bottoms = {}

        def rows_of_blocks(c):
            pair = slice(c, c + 2)
            bottom = turn_psum.tile([P, 2, BAND_ROWS, DETAIL_W], F32, tag="turned")
            bottoms[c] = bottom
            for v in range(2):
                nc.tensor.matmul(
                    out=bottom[:].rearrange("p c r j -> p (c r) j"),
                    lhsT=ident_bf[:],
                    rhs=pixels[:, pair, :, 1, :, v].rearrange("p c r j -> p (c r) j"),
                    start=(v == 0),
                    stop=(v == 1),
                )
            nc.vector.scalar_tensor_tensor(
                out=by_channel[:, pair, :, :],
                in0=pixels[:, pair, :, 0, :, 0],
                scalar=3.0,
                in1=pixels[:, pair, :, 0, :, 1],
                op0=ALU.mult,
                op1=ALU.subtract,
            )

        def join_rows(c):
            pair = slice(c, c + 2)
            nc.vector.tensor_tensor(out=by_channel[:, pair, :, :], in0=by_channel[:, pair, :, :], in1=bottoms[c][:], op=ALU.subtract)
            nc.scalar.activation(out=squares[:, pair, :, :], in_=by_channel[:, pair, :, :], func=ACT.Square)

        for c in range(0, CH, 2):
            rows_of_blocks(c)
            if c > 0:
                join_rows(c - 2)
        join_rows(CH - 2)
        def inner(band, rows, r):
            return band[rows, r, PAD : PAD + DETAIL_W, :].rearrange("p j c -> p (j c)")

        for r in range(BAND_ROWS):
            sorted_row = detail[:, r, PAD : PAD + DETAIL_W, :].rearrange("p j (h c) -> p h j c", h=2)
            row_by_channel = by_channel[:, :, r, :].rearrange("p (h c) j -> p h j c", h=2)
            if r % 2 == 0:
                nc.scalar.copy(out=sorted_row, in_=row_by_channel)
            else:
                nc.vector.tensor_copy(out=sorted_row, in_=row_by_channel)
            nc.sync.dma_start(out=inner(detail_up, slice(BATCH, P), r), in_=inner(detail, slice(0, P - BATCH), r))
            nc.sync.dma_start(out=inner(detail_dn, slice(0, P - BATCH), r), in_=inner(detail, slice(BATCH, P), r))
        for g in PASS_ORDER[EARLY_W:]:
            load_w(g)

        nc.vector.tensor_reduce(
            out=strip_sums[:, 0, 1:17], in_=by_channel[:].rearrange("p c r (e l) -> p e (c r) l", l=PAD), axis=AX.XY, op=ALU.add
        )
        nc.vector.tensor_reduce(
            out=strip_sums[:, 1, 1:17], in_=squares[:].rearrange("p c r (e l) -> p e (c r) l", l=PAD), axis=AX.XY, op=ALU.add
        )
        window_sums = keep.tile([P, 2, 2, GRID], F32)
        inner = strip_sums[:, :, 1:17].rearrange("p q (j v) -> p q j v", v=2)
        left = strip_sums[:, :, 0:16].rearrange("p q (j v) -> p q j v", v=2)
        right = strip_sums[:, :, 2:18].rearrange("p q (j v) -> p q j v", v=2)
        nc.vector.tensor_tensor(out=window_sums[:, 0, :, :], in0=inner[:, :, :, 0], in1=inner[:, :, :, 1], op=ALU.add)
        nc.vector.tensor_tensor(out=window_sums[:, 1, :, :], in0=left[:, :, :, 0], in1=right[:, :, :, 1], op=ALU.add)
        nc.vector.tensor_tensor(out=window_sums[:, 1, :, :], in0=window_sums[:, 1, :, :], in1=window_sums[:, 0, :, :], op=ALU.add)
        token_sums = turn_psum.tile([P, 2 * GRID], F32, tag="turned")
        nc.tensor.matmul(
            out=token_sums[:], lhsT=sum_own[:], rhs=window_sums[:, 0, :, :].rearrange("p q j -> p (q j)"), start=True, stop=False
        )
        nc.tensor.matmul(
            out=token_sums[:], lhsT=sum_near[:], rhs=window_sums[:, 1, :, :].rearrange("p q j -> p (q j)"), start=False, stop=True
        )
        regroup_w(PASS_ORDER[0], WIDE)
        regroup_w(PASS_ORDER[0], REST)
        mean = keep.tile([P, GRID], F32)
        mean_sq = keep.tile([P, GRID], F32)
        var = keep.tile([P, GRID], F32)
        std = keep.tile([P, GRID], F32)
        rstd0 = keep.tile([P, GRID], F32)
        newton = keep.tile([P, GRID], F32)
        rstd = keep.tile([P, GRID], F32)
        shift = keep.tile([P, GRID], F32)
        nc.vector.tensor_scalar(out=mean[:], in0=token_sums[:, 0:GRID], scalar1=1.0 / K, scalar2=None, op0=ALU.mult)
        nc.vector.tensor_scalar(out=var[:], in0=token_sums[:, GRID : 2 * GRID], scalar1=1.0 / K, scalar2=EPS, op0=ALU.mult, op1=ALU.add)
        nc.vector.tensor_tensor(out=mean_sq[:], in0=mean[:], in1=mean[:], op=ALU.mult)
        nc.vector.tensor_tensor(out=var[:], in0=var[:], in1=mean_sq[:], op=ALU.subtract)
        nc.scalar.activation(out=std[:], in_=var[:], func=ACT.Sqrt)
        nc.vector.reciprocal(out=rstd0[:], in_=std[:])
        nc.vector.tensor_tensor(out=newton[:], in0=var[:], in1=rstd0[:], op=ALU.mult)
        nc.vector.tensor_tensor(out=newton[:], in0=newton[:], in1=rstd0[:], op=ALU.mult)
        nc.vector.tensor_scalar(out=newton[:], in0=newton[:], scalar1=-0.5, scalar2=1.5, op0=ALU.mult, op1=ALU.add)
        nc.vector.tensor_tensor(out=rstd[:], in0=rstd0[:], in1=newton[:], op=ALU.mult)
        nc.vector.scalar_tensor_tensor(out=shift[:], in0=mean[:], scalar=-1.0, in1=rstd[:], op0=ALU.mult, op1=ALU.mult)
        regroup_w(PASS_ORDER[1], WIDE)
        regroup_w(PASS_ORDER[1], REST)
        quantise_w(PASS_ORDER[0])
        quantise_w(PASS_ORDER[1])

        normed = keep.tile([P, GRID, HALF_K], F32)
        normed_v = normed[:].rearrange("p j (r q s c) -> p j r q s c", r=BAND_ROWS, q=PATCH, s=VIEWS, c=CH)
        views = ((detail, 0), (detail_up, -PAD), (detail_up, PAD), (detail_dn, -PAD), (detail_dn, PAD))
        planes = keep.tile([P, SLOTS, J_GROUPS, GROUP_TOKENS], BF16, tag="image")

        def normalise(jq, s):
            source, dx = views[s]
            for j in range(jq * J_GROUP, (jq + 1) * J_GROUP):
                first = PAD + PATCH * j + dx
                if s == 0:
                    nc.scalar.activation(
                        out=normed_v[:, j, :, :, s, :],
                        in_=source[:, :, first : first + PATCH, :],
                        func=ACT.Identity,
                        scale=rstd[:, j : j + 1],
                        bias=shift[:, j : j + 1],
                    )
                else:
                    nc.vector.tensor_scalar(
                        out=normed_v[:, j, :, :, s, :],
                        in0=source[:, :, first : first + PATCH, :],
                        scalar1=rstd[:, j : j + 1],
                        scalar2=shift[:, j : j + 1],
                        op0=ALU.mult,
                        op1=ALU.add,
                    )

        turned_tiles = {}

        def turn(n):
            jq, sg = divmod(n, HALF_SLOTS)
            turned = turn_psum.tile([P, J_GROUP, P], F32)
            turned_tiles[n] = turned
            for j4 in range(J_GROUP):
                nc.tensor.transpose(
                    out=turned[:, j4, :], in_=normed[:, jq * J_GROUP + j4, sg * P : (sg + 1) * P], identity=turn_order[:]
                )

        def empty(n):
            jq, sg = divmod(n, HALF_SLOTS)
            for h in range(2):
                slot = sg + HALF_SLOTS * h
                nc.scalar.activation(
                    out=planes[:, slot, jq, :].rearrange("p (g j) -> p g j", j=J_GROUP),
                    in_=turned_tiles[n][:, :, 64 * h : 64 * h + 64].rearrange("p j g -> p g j"),
                    func=ACT.Identity,
                    scale=gain_t[:, slot : slot + 1],
                    bias=gain_t[:, 32 + slot : 33 + slot],
                )

        z_grps = {}

        def regroup_z(jq, g):
            z_grp = z_grp_pool.tile([P, GROUP_TOKENS, PACK], BF16, align_bytes=64)
            z_grps[(jq, g)] = z_grp
            nc.vector.tensor_copy(
                out=z_grp[:].rearrange("p (w i) t -> p w t i", i=4),
                in_=planes[:, PACK * g : PACK * (g + 1), jq, :].rearrange("p t (w i) -> p w t i", i=4),
            )

        def quantise_z(jq, g):
            toks = slice(jq * GROUP_TOKENS, (jq + 1) * GROUP_TOKENS)
            nc.vector.quantize_mx(
                out=z_codes[:, g, toks].bitcast(FP8X4),
                scales=z_scales[:, g, toks],
                in_=z_grps[(jq, g)][:].rearrange("p w t -> p (w t)"),
            )

        def passes_done_at(n):
            return [(n // HALF_SLOTS, g) for g in PASS_ORDER if 0 <= n < STEPS and LAST_PLANE[g] == n % HALF_SLOTS]

        accs = {}

        def multiply(jq, g):
            for bh in range(2):
                m = 2 * jq + bh
                rows = slice(m * P, (m + 1) * P)
                if g == PASS_ORDER[0]:
                    acc_wide = acc_psum.tile([P, N_WIDE], F32, tag="wide%d" % bh)
                    acc_rest = acc_psum.tile([P, DIM - N_WIDE], F32, tag="rest%d" % bh)
                    accs[m] = ((acc_wide, WIDE), (acc_rest, REST))
                for acc, cols in accs[m]:
                    nc.tensor.matmul_mx(
                        out=acc[:],
                        lhsT=z_codes[:, g, rows].bitcast(FP8X4),
                        lhsT_scale=z_scales[:, g, rows],
                        rhs=w_codes[:, g, cols].bitcast(FP8X4),
                        rhs_scale=w_scales[:, g, cols],
                        start=(g == PASS_ORDER[0]),
                        stop=(g == PASS_ORDER[-1]),
                    )
                if g == PASS_ORDER[-1]:
                    for acc, cols in accs[m]:
                        nc.vector.tensor_tensor(out=tok_bias[:, m, cols], in0=acc[:], in1=tok_bias[:, m, cols], op=ALU.add)
                        nc.sync.dma_start(out=token_rows(out, m)[:, :, cols], in_=tok_bias[:, m, cols])

        normalise(0, 0)
        normalise(1, 0)
        for jq in range(J_GROUPS):
            for s in range(1, VIEWS):
                normalise(jq, s)
        regroup_w(PASS_ORDER[3], WIDE)
        regroup_w(PASS_ORDER[3], REST)
        quantise_w(PASS_ORDER[3])
        for n in range(AHEAD):
            turn(n)
        for n in range(STEPS + LAG):
            if n + AHEAD < STEPS:
                turn(n + AHEAD)
            if n < STEPS:
                empty(n)
            for jq, g in passes_done_at(n):
                regroup_z(jq, g)
            for jq, g in passes_done_at(n - 1):
                quantise_z(jq, g)
            if n == W_STEP:
                regroup_w(PASS_ORDER[2], WIDE)
                regroup_w(PASS_ORDER[2], REST)
            if n == W_STEP + 2:
                quantise_w(PASS_ORDER[2])
                regroup_w(PASS_ORDER[4], WIDE)
                regroup_w(PASS_ORDER[4], REST)
                quantise_w(PASS_ORDER[4])
            for jq, g in passes_done_at(n - LAG):
                multiply(jq, g)
